import numpy as np
import ml_dtypes


def mxq(x, axis, fmt="e4m3"):
    dtype, down = {"e4m3": (ml_dtypes.float8_e4m3fn, 7), "e5m2": (ml_dtypes.float8_e5m2, 14)}[fmt]
    v = np.moveaxis(np.asarray(x, np.float32).astype(ml_dtypes.bfloat16).astype(np.float64), axis, -1)
    blocks = v.reshape(v.shape[:-1] + (-1, 32))
    amax = np.abs(blocks).max(-1, keepdims=True)
    byte = np.maximum(np.where(amax > 0, np.frexp(amax)[1] - 1 + 127, 0) - down, 1)
    scale = np.exp2(byte - 127.0)
    codes = (blocks / scale).astype(np.float32).astype(dtype).astype(np.float64)
    return np.moveaxis((codes * scale).reshape(v.shape), -1, axis)


WIDE = False


def mx_kscale(k):
    if not WIDE:
        return np.ones(k)
    levels = np.array([10, -10, 5, -5, 0])
    a = np.random.permutation(np.resize(levels, k // 512 * 4)).reshape(k // 512, 4)
    idx = np.arange(k)
    return np.exp2(a[idx // 512, idx % 128 // 32])


BF16 = ml_dtypes.bfloat16


def bf(x):
    return np.asarray(x, np.float32).astype(BF16)


def f64(x):
    return np.asarray(x).astype(np.float64)


B, S_IMG, S_TXT, D, H, HD = 1, 3072, 1024, 1024, 2, 128
S = S_TXT + S_IMG
E = H * HD
EPS = 1e-5


def rmsnorm(x, w):
    var = np.mean(np.square(x), axis=-1, keepdims=True)
    return x * (1.0 / np.sqrt(var + EPS)) * w


def rope(x, cos, sin):
    xr = x.reshape(x.shape[:-1] + (HD // 2, 2))
    x_rot = np.stack([-xr[..., 1], xr[..., 0]], axis=-1).reshape(x.shape)
    return x * cos[None, :, None, :] + x_rot * sin[None, :, None, :]


def setup_inputs():
    r = np.random.standard_normal
    s, u = mx_kscale(D), mx_kscale(D)
    pw = 0.015 / np.sqrt(D)
    return {"hidden_states": bf(r((B, S_IMG, D)) * s),
            "encoder_hidden_states": bf(r((B, S_TXT, D)) * u),
            "rope_cos": bf(np.random.uniform(size=(S, HD))),
            "rope_sin": bf(np.random.uniform(size=(S, HD))),
            "Wq": bf(r((E, D)) * pw / s),
            "Wk": bf(r((E, D)) * pw / s),
            "Waq": bf(r((E, D)) * pw / u),
            "baq": bf(r(E) * 0.005),
            "Wak": bf(r((E, D)) * pw / u),
            "bak": bf(r(E) * 0.005),
            "wq_norm": bf(1.75 + 0.15 * r(HD)),
            "wk_norm": bf(1.75 + 0.15 * r(HD)),
            "waq_norm": bf(1.75 + 0.15 * r(HD)),
            "wak_norm": bf(1.75 + 0.15 * r(HD))}


def reference(hidden_states, encoder_hidden_states, rope_cos, rope_sin, Wq, Wk, Waq, baq, Wak, bak, wq_norm, wk_norm, waq_norm, wak_norm):
    xq = mxq(f64(hidden_states), 2, "e4m3")
    cq = mxq(f64(encoder_hidden_states), 2, "e4m3")
    q = (xq @ mxq(f64(Wq).T, 0, "e4m3")).reshape(B, S_IMG, H, HD)
    k = (xq @ mxq(f64(Wk).T, 0, "e4m3")).reshape(B, S_IMG, H, HD)
    q = rmsnorm(q, f64(wq_norm))
    k = rmsnorm(k, f64(wk_norm))
    eq = ((cq @ mxq(f64(Waq).T, 0, "e4m3")) + f64(baq)).reshape(B, S_TXT, H, HD)
    ek = ((cq @ mxq(f64(Wak).T, 0, "e4m3")) + f64(bak)).reshape(B, S_TXT, H, HD)
    eq = rmsnorm(eq, f64(waq_norm))
    ek = rmsnorm(ek, f64(wak_norm))
    q = np.concatenate([eq, q], axis=1)
    k = np.concatenate([ek, k], axis=1)
    return rope(q, f64(rope_cos), f64(rope_sin)), rope(k, f64(rope_cos), f64(rope_sin))

@@ -1,0 +1,334 @@
+from contextlib import ExitStack
+
+import concourse.mybir as mybir
+from concourse.masks import make_identity
+
+F32 = mybir.dt.float32
+BF16 = mybir.dt.bfloat16
+U32 = mybir.dt.uint32
+U8 = mybir.dt.uint8
+FP8X4 = mybir.dt.float8_e4m3fn_x4
+ACT = mybir.ActivationFunctionType
+ALU = mybir.AluOpType
+
+P = 128
+K = 1024
+PASSES = 2
+BLOCKS = 4
+HEAD = 128
+HALF = 64
+OUTS = 512
+S_TXT = 1024
+S_IMG = 3072
+EPS = 1e-5
+PAIR = 2
+AHEAD = 2
+
+FLOPS = 2 * (S_TXT + S_IMG) * K * OUTS
+
+
+def tile_flux2attention_pa_t_kernel(
+    tc,
+    hidden_states,
+    encoder_hidden_states,
+    rope_cos,
+    rope_sin,
+    Wq,
+    Wk,
+    Waq,
+    baq,
+    Wak,
+    bak,
+    wq_norm,
+    wk_norm,
+    waq_norm,
+    wak_norm,
+    out_0,
+    out_1,
+):
+    nc = tc.nc
+    TXT, IMG = 0, 1
+    first_row = (0, S_TXT)
+    n_tiles = (S_TXT // P, S_IMG // P)
+    weights = ((Waq, Wak), (Wq, Wk))
+
+    def by_partition(rows, stream):
+        lo = first_row[stream]
+        return rows[lo : lo + n_tiles[stream] * P, :].rearrange("(p m) c -> p m c", p=P)
+
+    x_dram = (
+        encoder_hidden_states.rearrange("b (p m) k -> p (b m) k", p=P),
+        hidden_states.rearrange("b (p m) k -> p (b m) k", p=P),
+    )
+    q_rows = out_0.rearrange("b s h d -> (b s) (h d)")
+    k_rows = out_1.rearrange("b s h d -> (b s) (h d)")
+    q_dram = (by_partition(q_rows, TXT), by_partition(q_rows, IMG))
+    k_dram = (by_partition(k_rows, TXT), by_partition(k_rows, IMG))
+
+    pairs = [(s, m) for s in (TXT, IMG) for m in range(0, n_tiles[s], PAIR)]
+
+    with ExitStack() as ctx:
+        const = ctx.enter_context(tc.tile_pool(name="const", bufs=1))
+        x_pool = ctx.enter_context(tc.tile_pool(name="x_pool", bufs=len(pairs)))
+        w_pool = ctx.enter_context(tc.tile_pool(name="w_pool", bufs=8))
+        group_pool = ctx.enter_context(tc.tile_pool(name="group_pool", bufs=2))
+        code_pool = ctx.enter_context(tc.tile_pool(name="code_pool", bufs=4))
+        table_pool = ctx.enter_context(tc.tile_pool(name="table_pool", bufs=16))
+        work = ctx.enter_context(tc.tile_pool(name="work", bufs=3))
+        out_pool = ctx.enter_context(tc.tile_pool(name="out_pool", bufs=4))
+        psum_t = ctx.enter_context(tc.psum_pool(name="psum_t", bufs=4))
+        psum_y = ctx.enter_context(tc.psum_pool(name="psum_y", bufs=4))
+
+        w_raw = {}
+        x_raw = {}
+        trig = {}
+
+        def load_weights(stream):
+            for qk in range(2):
+                for h in range(2):
+                    t = w_pool.tile([P, K], BF16, name="w_raw%d%d%d" % (stream, qk, h), tag="w_raw")
+                    nc.sync.dma_start(out=t[:], in_=weights[stream][qk][h * HEAD : (h + 1) * HEAD, :])
+                    w_raw[(stream, qk, h)] = t
+
+        def load_pair(i):
+            stream, m = pairs[i]
+            t = x_pool.tile([P, PAIR, K], BF16, name="x_raw%d" % i, tag="x_raw")
+            nc.sync.dma_start(out=t[:], in_=x_dram[stream][:, m : m + PAIR, :])
+            x_raw[i] = t
+
+        def load_trig(stream):
+            for name, table in (("cos", rope_cos), ("sin", rope_sin)):
+                t = const.tile([P, n_tiles[stream], HEAD], BF16, name="%s%d" % (name, stream))
+                nc.sync.dma_start(out=t[:], in_=by_partition(table, stream))
+                trig[(name, stream)] = t
+
+        load_weights(TXT)
+        load_pair(0)
+        load_trig(TXT)
+        load_pair(1)
+        load_pair(2)
+        load_pair(3)
+        load_weights(IMG)
+        load_trig(IMG)
+        for i in range(4, len(pairs)):
+            load_pair(i)
+
+        ident = const.tile([P, P], F32)
+        make_identity(nc, ident[:])
+        to_planes = const.tile([P, P], F32)
+        nc.vector.tensor_copy(
+            out=to_planes[:].rearrange("r (two i) -> r two i", two=2),
+            in_=ident[:].rearrange("r (i two) -> r two i", two=2),
+        )
+
+        ones = const.tile([P, P], BF16)
+        nc.vector.memset(ones[:], 1.0)
+        rows = const.tile([P, 2 * OUTS], BF16)
+        nc.vector.memset(rows[:], 0.0)
+        col = 0
+        for vec in (waq_norm, wak_norm, wq_norm, wk_norm, baq, bak):
+            n = vec.shape[0]
+            nc.scalar.dma_start(out=rows[0:1, col : col + n], in_=vec.unsqueeze(0))
+            col += n
+        gains_ps = psum_y.tile([P, 4, HEAD], F32, tag="y")
+        nc.tensor.matmul(
+            out=gains_ps[:].rearrange("p v c -> p (v c)"), lhsT=ones[:], rhs=rows[:, 0:OUTS], start=True, stop=True
+        )
+        bias_ps = psum_y.tile([P, 4, HEAD], F32, tag="y")
+        nc.tensor.matmul(
+            out=bias_ps[:].rearrange("p v c -> p (v c)"), lhsT=ones[:], rhs=rows[:, OUTS : 2 * OUTS], start=True, stop=True
+        )
+        gain_cos = {}
+        gain_sin = {}
+        for stream in (TXT, IMG):
+            g = gains_ps[:, 2 * stream : 2 * stream + 2, :].rearrange("p v (i two) -> p v two i", two=2)
+            gc = const.tile([P, 2, 2, HALF], F32, name="gain_cos%d" % stream)
+            nc.vector.tensor_copy(out=gc[:], in_=g)
+            gs = const.tile([P, 2, 2, HALF], F32, name="gain_sin%d" % stream)
+            nc.vector.tensor_scalar_mul(out=gs[:, :, 0, :], in0=g[:, :, 1, :], scalar1=-1.0)
+            nc.vector.tensor_copy(out=gs[:, :, 1, :], in_=g[:, :, 0, :])
+            gain_cos[stream] = gc
+            gain_sin[stream] = gs
+        bias = const.tile([P, 4, 2, HALF], F32)
+        nc.vector.tensor_copy(out=bias[:], in_=bias_ps[:].rearrange("p v (i two) -> p v two i", two=2))
+
+        w_codes = {}
+        w_scales = {}
+
+        def prepare_weights(stream):
+            grouped = group_pool.tile([P, PASSES, OUTS, 4], BF16, align_bytes=64, name="w_grouped", bufs=1)
+            grouped_words = grouped[:].bitcast(F32)
+            for qk in range(2):
+                for h in range(2):
+                    head = 2 * qk + h
+                    words = w_raw[(stream, qk, h)][:].bitcast(F32)
+                    wt = psum_t.tile([P, BLOCKS, P], F32, tag="t")
+                    for c in range(BLOCKS):
+                        nc.tensor.transpose(wt[:, c, :], words[:, c * P : (c + 1) * P], to_planes[:])
+                    nc.scalar.copy(
+                        out=grouped_words[:, :, head * HEAD : (head + 1) * HEAD, :],
+                        in_=wt[:].rearrange("p (g u) r -> p g r u", u=2),
+                    )
+            codes = const.tile([P, PASSES, OUTS], U32, align_bytes=64, name="w_codes%d" % stream)
+            scales = const.tile([P, PASSES, OUTS], U8, align_bytes=64, name="w_scales%d" % stream)
+            nc.vector.quantize_mx(
+                out=codes[:].rearrange("p g c -> p (g c)").bitcast(FP8X4),
+                scales=scales[:].rearrange("p g c -> p (g c)"),
+                in_=grouped[:].rearrange("p g c j -> p (g c j)"),
+            )
+            w_codes[stream] = codes
+            w_scales[stream] = scales
+
+        x_grouped = {}
+        x_t = {}
+        x_codes = {}
+        x_scales = {}
+        tables = {}
+        y_ps = {}
+
+        def transpose_pair(i):
+            grouped = group_pool.tile([P, PAIR, PASSES, P, 4], BF16, align_bytes=64, name="x_grouped")
+            for n in range(PAIR):
+                words = x_raw[i][:, n, :].bitcast(F32)
+                xt = psum_t.tile([P, BLOCKS, P], F32, tag="t")
+                for c in range(BLOCKS):
+                    nc.tensor.transpose(xt[:, c, :], words[:, c * P : (c + 1) * P], ident[:])
+                x_t[(i, n)] = xt
+            x_grouped[i] = grouped
+
+        def regroup(i, n):
+            nc.scalar.copy(
+                out=x_grouped[i][:, n].bitcast(F32),
+                in_=x_t[(i, n)][:].rearrange("p (g u) t -> p g t u", u=2),
+            )
+
+        def quantise_pair(i):
+            codes = code_pool.tile([P, PAIR, PASSES, P], U32, align_bytes=64, name="x_codes")
+            scales = code_pool.tile([P, PAIR, PASSES, P], U8, align_bytes=64, name="x_scales")
+            nc.vector.quantize_mx(
+                out=codes[:].rearrange("p n g t -> p (n g t)").bitcast(FP8X4),
+                scales=scales[:].rearrange("p n g t -> p (n g t)"),
+                in_=x_grouped[i][:].rearrange("p n g t j -> p (n g t j)"),
+            )
+            x_codes[i] = codes
+            x_scales[i] = scales
+
+        def make_tables(i):
+            stream, m = pairs[i]
+            for n in range(PAIR):
+                tab = table_pool.tile([P, 2, 2, 2, HALF], F32, name="tab")
+                for cs, name, gain in ((0, "cos", gain_cos), (1, "sin", gain_sin)):
+                    planes = trig[(name, stream)][:, m + n, :].rearrange("p (i two) -> p two i", two=2)
+                    nc.gpsimd.tensor_tensor(
+                        out=tab[:, cs],
+                        in0=planes.unsqueeze(1).to_broadcast([P, 2, 2, HALF]),
+                        in1=gain[stream][:],
+                        op=ALU.mult,
+                    )
+                tables[(i, n)] = tab
+
+        def project_pair(i):
+            stream = pairs[i][0]
+            for n in range(PAIR):
+                y = psum_y.tile([P, 4, HEAD], F32, tag="y")
+                for g in range(PASSES):
+                    nc.tensor.matmul_mx(
+                        out=y[:].rearrange("p v c -> p (v c)"),
+                        lhsT=x_codes[i][:, n, g, :].bitcast(FP8X4),
+                        lhsT_scale=x_scales[i][:, n, g, :],
+                        rhs=w_codes[stream][:, g, :].bitcast(FP8X4),
+                        rhs_scale=w_scales[stream][:, g, :],
+                        start=(g == 0),
+                        stop=(g == PASSES - 1),
+                    )
+                y_ps[(i, n)] = y
+
+        rstd = {}
+
+        def add_bias(i, n):
+            if pairs[i][0] == TXT:
+                yb = work.tile([P, 4, HEAD], F32, name="yb")
+                nc.vector.tensor_tensor(
+                    out=yb[:], in0=y_ps[(i, n)][:], in1=bias[:].rearrange("p v two i -> p v (two i)"), op=ALU.add
+                )
+                y_ps[(i, n)] = yb
+
+        def inverse_rms(i, n):
+            y = y_ps[(i, n)]
+            squares = work.tile([P, 4, HEAD], BF16, name="squares")
+            sumsq = work.tile([P, 4], F32, name="sumsq")
+            for v in range(4):
+                nc.scalar.activation(
+                    out=squares[:, v, :], in_=y[:, v, :], func=ACT.Square, accum_out=sumsq[:, v : v + 1]
+                )
+            r = work.tile([P, 4], F32, name="r")
+            nc.scalar.activation(out=r[:], in_=sumsq[:], func=ACT.Abs_reciprocal_sqrt, bias=EPS, scale=1.0 / HEAD)
+            rstd[(i, n)] = r
+
+        rotated = {}
+
+        def rotate(i, n):
+            tab = tables[(i, n)]
+            y4 = y_ps[(i, n)][:].rearrange("p (q h) c -> p q h c", q=2)
+            straight = work.tile([P, 2, 2, HEAD], F32, name="straight")
+            nc.vector.tensor_tensor(
+                out=straight[:],
+                in0=y4,
+                in1=tab[:, 0].rearrange("p q two i -> p q (two i)").unsqueeze(2).to_broadcast([P, 2, 2, HEAD]),
+                op=ALU.mult,
+            )
+            crossed = work.tile([P, 2, 2, HEAD], F32, name="crossed")
+            for two in range(2):
+                here = slice(two * HALF, (two + 1) * HALF)
+                there = slice((1 - two) * HALF, (2 - two) * HALF)
+                nc.vector.tensor_tensor(
+                    out=crossed[:, :, :, here],
+                    in0=y4[:, :, :, there],
+                    in1=tab[:, 1, :, two, :].unsqueeze(2).to_broadcast([P, 2, 2, HALF]),
+                    op=ALU.mult,
+                )
+            rot = work.tile([P, 4, HEAD], F32, name="rot")
+            nc.vector.tensor_tensor(
+                out=rot[:].rearrange("p (q h) c -> p q h c", q=2), in0=straight[:], in1=crossed[:], op=ALU.add
+            )
+            rotated[(i, n)] = rot
+
+        def scale_and_store(i, n):
+            stream, m = pairs[i]
+            result = out_pool.tile([P, 4, HEAD], F32, name="result")
+            for v in range(4):
+                nc.scalar.activation(
+                    out=result[:, v, :].rearrange("p (i two) -> p i two", two=2),
+                    in_=rotated[(i, n)][:, v, :].rearrange("p (two i) -> p i two", two=2),
+                    func=ACT.Copy,
+                    scale=rstd[(i, n)][:, v : v + 1],
+                )
+            nc.sync.dma_start(out=q_dram[stream][:, m + n, :], in_=result[:, 0:2, :].rearrange("p h c -> p (h c)"))
+            nc.sync.dma_start(out=k_dram[stream][:, m + n, :], in_=result[:, 2:4, :].rearrange("p h c -> p (h c)"))
+
+        tiles = [(i, n) for i in range(len(pairs)) for n in range(PAIR)]
+        for step in range(-AHEAD, len(pairs)):
+            ahead = step + AHEAD
+            if ahead < len(pairs):
+                if pairs[ahead][1] == 0:
+                    prepare_weights(pairs[ahead][0])
+                transpose_pair(ahead)
+                make_tables(ahead)
+            if 0 <= step + 1 < len(pairs):
+                project_pair(step + 1)
+            if step == -1:
+                add_bias(0, 0)
+                inverse_rms(0, 0)
+            for n in range(PAIR):
+                if step >= 0:
+                    t = PAIR * step + n
+                    if t + 1 < len(tiles):
+                        add_bias(*tiles[t + 1])
+                        inverse_rms(*tiles[t + 1])
+                    rotate(step, n)
+                if ahead < len(pairs):
+                    regroup(ahead, n)
+                if step >= 0:
+                    scale_and_store(step, n)
+            if ahead < len(pairs):
+                quantise_pair(ahead)

@@ -22,7 +22,6 @@ S_TXT = 1024
 S_IMG = 3072
 EPS = 1e-5
 PAIR = 2
-AHEAD = 2
 
 FLOPS = 2 * (S_TXT + S_IMG) * K * OUTS
 
@@ -50,11 +49,12 @@ def tile_flux2attention_pa_t_kernel(
     TXT, IMG = 0, 1
     first_row = (0, S_TXT)
     n_tiles = (S_TXT // P, S_IMG // P)
+    first_tile = (0, S_TXT // P)
     weights = ((Waq, Wak), (Wq, Wk))
 
-    def by_partition(rows, stream):
+    def by_partition(table, stream):
         lo = first_row[stream]
-        return rows[lo : lo + n_tiles[stream] * P, :].rearrange("(p m) c -> p m c", p=P)
+        return table[lo : lo + n_tiles[stream] * P, :].rearrange("(p m) c -> p m c", p=P)
 
     x_dram = (
         encoder_hidden_states.rearrange("b (p m) k -> p (b m) k", p=P),
@@ -65,19 +65,27 @@ def tile_flux2attention_pa_t_kernel(
     q_dram = (by_partition(q_rows, TXT), by_partition(q_rows, IMG))
     k_dram = (by_partition(k_rows, TXT), by_partition(k_rows, IMG))
 
-    pairs = [(s, m) for s in (TXT, IMG) for m in range(0, n_tiles[s], PAIR)]
+    tiles = [(s, m) for s in (TXT, IMG) for m in range(n_tiles[s])]
+    n_pairs = len(tiles) // PAIR
 
     with ExitStack() as ctx:
         const = ctx.enter_context(tc.tile_pool(name="const", bufs=1))
-        x_pool = ctx.enter_context(tc.tile_pool(name="x_pool", bufs=len(pairs)))
+        x_pool = ctx.enter_context(tc.tile_pool(name="x_pool", bufs=n_pairs))
         w_pool = ctx.enter_context(tc.tile_pool(name="w_pool", bufs=8))
-        group_pool = ctx.enter_context(tc.tile_pool(name="group_pool", bufs=2))
-        code_pool = ctx.enter_context(tc.tile_pool(name="code_pool", bufs=4))
-        table_pool = ctx.enter_context(tc.tile_pool(name="table_pool", bufs=16))
-        work = ctx.enter_context(tc.tile_pool(name="work", bufs=3))
-        out_pool = ctx.enter_context(tc.tile_pool(name="out_pool", bufs=4))
-        psum_t = ctx.enter_context(tc.psum_pool(name="psum_t", bufs=4))
+        ring3 = ctx.enter_context(tc.tile_pool(name="ring3", bufs=3))
+        ring4 = ctx.enter_context(tc.tile_pool(name="ring4", bufs=4))
+        ring6 = ctx.enter_context(tc.tile_pool(name="ring6", bufs=6))
+        table_pool = ctx.enter_context(tc.tile_pool(name="table_pool", bufs=S_TXT // P + 1))
+        psum_g = ctx.enter_context(tc.psum_pool(name="psum_g", bufs=1))
+        psum_t = ctx.enter_context(tc.psum_pool(name="psum_t", bufs=3))
         psum_y = ctx.enter_context(tc.psum_pool(name="psum_y", bufs=4))
+
+        vectors = const.tile([1, 2 * OUTS], BF16)
+        col = 0
+        for vec in (waq_norm, wak_norm, wq_norm, wk_norm, baq, bak):
+            n = vec.shape[0]
+            nc.scalar.dma_start(out=vectors[:, col : col + n], in_=vec.unsqueeze(0))
+            col += n
 
         w_raw = {}
         x_raw = {}
@@ -85,250 +93,275 @@ def tile_flux2attention_pa_t_kernel(
 
         def load_weights(stream):
             for qk in range(2):
-                for h in range(2):
-                    t = w_pool.tile([P, K], BF16, name="w_raw%d%d%d" % (stream, qk, h), tag="w_raw")
-                    nc.sync.dma_start(out=t[:], in_=weights[stream][qk][h * HEAD : (h + 1) * HEAD, :])
-                    w_raw[(stream, qk, h)] = t
+                by_parity = weights[stream][qk].rearrange("(hi two) k -> two hi k", two=2)
+                for two in range(2):
+                    t = w_pool.tile([P, K], BF16, name="w_raw%d%d%d" % (stream, qk, two), tag="w_raw")
+                    nc.sync.dma_start(out=t[:], in_=by_parity[two])
+                    w_raw[(stream, 2 * qk + two)] = t
 
-        def load_pair(i):
-            stream, m = pairs[i]
-            t = x_pool.tile([P, PAIR, K], BF16, name="x_raw%d" % i, tag="x_raw")
+        def load_pair(pair):
+            stream, m = tiles[PAIR * pair]
+            t = x_pool.tile([P, PAIR, K], BF16, name="x_raw%d" % pair, tag="x_raw")
             nc.sync.dma_start(out=t[:], in_=x_dram[stream][:, m : m + PAIR, :])
-            x_raw[i] = t
+            x_raw[pair] = t
 
         def load_trig(stream):
-            for name, table in (("cos", rope_cos), ("sin", rope_sin)):
-                t = const.tile([P, n_tiles[stream], HEAD], BF16, name="%s%d" % (name, stream))
-                nc.sync.dma_start(out=t[:], in_=by_partition(table, stream))
-                trig[(name, stream)] = t
+            t = const.tile([P, n_tiles[stream], 2, HEAD], BF16, name="trig%d" % stream)
+            nc.sync.dma_start(out=t[:, :, 0, :], in_=by_partition(rope_cos, stream))
+            nc.sync.dma_start(out=t[:, :, 1, :], in_=by_partition(rope_sin, stream))
+            trig[stream] = t
 
+        load_trig(TXT)
         load_weights(TXT)
         load_pair(0)
-        load_trig(TXT)
         load_pair(1)
         load_pair(2)
         load_pair(3)
         load_weights(IMG)
+        load_pair(4)
         load_trig(IMG)
-        for i in range(4, len(pairs)):
-            load_pair(i)
+        for pair in range(5, n_pairs):
+            load_pair(pair)
 
         ident = const.tile([P, P], F32)
         make_identity(nc, ident[:])
-        to_planes = const.tile([P, P], F32)
-        nc.vector.tensor_copy(
-            out=to_planes[:].rearrange("r (two i) -> r two i", two=2),
-            in_=ident[:].rearrange("r (i two) -> r two i", two=2),
-        )
 
         ones = const.tile([P, P], BF16)
         nc.vector.memset(ones[:], 1.0)
-        rows = const.tile([P, 2 * OUTS], BF16)
-        nc.vector.memset(rows[:], 0.0)
-        col = 0
-        for vec in (waq_norm, wak_norm, wq_norm, wk_norm, baq, bak):
-            n = vec.shape[0]
-            nc.scalar.dma_start(out=rows[0:1, col : col + n], in_=vec.unsqueeze(0))
-            col += n
-        gains_ps = psum_y.tile([P, 4, HEAD], F32, tag="y")
-        nc.tensor.matmul(
-            out=gains_ps[:].rearrange("p v c -> p (v c)"), lhsT=ones[:], rhs=rows[:, 0:OUTS], start=True, stop=True
-        )
-        bias_ps = psum_y.tile([P, 4, HEAD], F32, tag="y")
-        nc.tensor.matmul(
-            out=bias_ps[:].rearrange("p v c -> p (v c)"), lhsT=ones[:], rhs=rows[:, OUTS : 2 * OUTS], start=True, stop=True
-        )
-        gain_cos = {}
-        gain_sin = {}
+        ordered = const.tile([P, 3, OUTS], BF16)
+        nc.vector.memset(ordered[:], 0.0)
         for stream in (TXT, IMG):
-            g = gains_ps[:, 2 * stream : 2 * stream + 2, :].rearrange("p v (i two) -> p v two i", two=2)
-            gc = const.tile([P, 2, 2, HALF], F32, name="gain_cos%d" % stream)
-            nc.vector.tensor_copy(out=gc[:], in_=g)
-            gs = const.tile([P, 2, 2, HALF], F32, name="gain_sin%d" % stream)
-            nc.vector.tensor_scalar_mul(out=gs[:, :, 0, :], in0=g[:, :, 1, :], scalar1=-1.0)
-            nc.vector.tensor_copy(out=gs[:, :, 1, :], in_=g[:, :, 0, :])
-            gain_cos[stream] = gc
-            gain_sin[stream] = gs
-        bias = const.tile([P, 4, 2, HALF], F32)
-        nc.vector.tensor_copy(out=bias[:], in_=bias_ps[:].rearrange("p v (i two) -> p v two i", two=2))
+            w = vectors[:, 2 * HEAD * stream : 2 * HEAD * (stream + 1)].rearrange(
+                "p (q i two) -> p q two i", q=2, two=2
+            )
+            g = ordered[0:1, stream, :].rearrange("p (q two cs i) -> p q two cs i", q=2, two=2, cs=2)
+            nc.vector.tensor_copy(out=g[:, :, :, 0, :], in_=w)
+            nc.vector.tensor_scalar_mul(out=g[:, :, 0, 1, :], in0=w[:, :, 1, :], scalar1=-1.0)
+            nc.vector.tensor_copy(out=g[:, :, 1, 1, :], in_=w[:, :, 0, :])
+        for qk in range(2):
+            lo = qk * 2 * HEAD
+            nc.vector.tensor_copy(
+                out=ordered[0:1, 2, lo : lo + 2 * HEAD].rearrange("p (two h i) -> p two h i", two=2, h=2),
+                in_=vectors[:, OUTS + lo : OUTS + lo + 2 * HEAD].rearrange("p (h i two) -> p two h i", h=2, two=2),
+            )
+        gains = psum_g.tile([P, 2, OUTS], BF16)
+        for stream in (TXT, IMG):
+            nc.tensor.matmul(out=gains[:, stream, :], lhsT=ones[:], rhs=ordered[:, stream, :], start=True, stop=True)
+        bias_ps = psum_y.tile([P, OUTS], F32, tag="y")
+        nc.tensor.matmul(out=bias_ps[:], lhsT=ones[:], rhs=ordered[:, 2, :], start=True, stop=True)
+        bias = const.tile([P, OUTS], F32)
+        nc.vector.tensor_copy(out=bias[:], in_=bias_ps[:])
 
+        w_grouped = {}
         w_codes = {}
         w_scales = {}
+        x_t = {}
+        x_grouped = {}
+        x_codes = {}
+        x_scales = {}
+        table = {}
+        y = {}
+        rstd_in = {}
+        rstd = {}
+        straight = {}
+        crossed = {}
+        rotated = {}
 
-        def prepare_weights(stream):
-            grouped = group_pool.tile([P, PASSES, OUTS, 4], BF16, align_bytes=64, name="w_grouped", bufs=1)
-            grouped_words = grouped[:].bitcast(F32)
-            for qk in range(2):
-                for h in range(2):
-                    head = 2 * qk + h
-                    words = w_raw[(stream, qk, h)][:].bitcast(F32)
-                    wt = psum_t.tile([P, BLOCKS, P], F32, tag="t")
-                    for c in range(BLOCKS):
-                        nc.tensor.transpose(wt[:, c, :], words[:, c * P : (c + 1) * P], to_planes[:])
-                    nc.scalar.copy(
-                        out=grouped_words[:, :, head * HEAD : (head + 1) * HEAD, :],
-                        in_=wt[:].rearrange("p (g u) r -> p g r u", u=2),
-                    )
+        def is_tile(t):
+            return 0 <= t < len(tiles)
+
+        def is_pair(pair):
+            return 0 <= pair < n_pairs
+
+        def transpose_weight_plane(stream, plane):
+            if plane == 0:
+                w_grouped[stream] = const.tile([P, PASSES, OUTS, 4], BF16, align_bytes=64, name="w_grouped", tag="w_grouped")
+            words = w_raw[(stream, plane)][:].bitcast(F32)
+            wt = psum_t.tile([P, BLOCKS, P], F32, tag="t")
+            for c in range(BLOCKS):
+                nc.tensor.transpose(wt[:, c, :], words[:, c * P : (c + 1) * P], ident[:])
+            nc.scalar.copy(
+                out=w_grouped[stream][:].bitcast(F32)[:, :, plane * P : (plane + 1) * P, :],
+                in_=wt[:].rearrange("p (g u) r -> p g r u", u=2),
+            )
+
+        def quantise_weights(stream):
             codes = const.tile([P, PASSES, OUTS], U32, align_bytes=64, name="w_codes%d" % stream)
             scales = const.tile([P, PASSES, OUTS], U8, align_bytes=64, name="w_scales%d" % stream)
             nc.vector.quantize_mx(
                 out=codes[:].rearrange("p g c -> p (g c)").bitcast(FP8X4),
                 scales=scales[:].rearrange("p g c -> p (g c)"),
-                in_=grouped[:].rearrange("p g c j -> p (g c j)"),
+                in_=w_grouped[stream][:].rearrange("p g c j -> p (g c j)"),
             )
             w_codes[stream] = codes
             w_scales[stream] = scales
 
-        x_grouped = {}
-        x_t = {}
-        x_codes = {}
-        x_scales = {}
-        tables = {}
-        y_ps = {}
-
-        def transpose_pair(i):
-            grouped = group_pool.tile([P, PAIR, PASSES, P, 4], BF16, align_bytes=64, name="x_grouped")
+        def transpose_pair(pair):
+            if not is_pair(pair):
+                return
+            x_grouped[pair] = ring3.tile([P, PAIR, PASSES, P, 4], BF16, align_bytes=64, name="x_grouped")
             for n in range(PAIR):
-                words = x_raw[i][:, n, :].bitcast(F32)
+                words = x_raw[pair][:, n, :].bitcast(F32)
                 xt = psum_t.tile([P, BLOCKS, P], F32, tag="t")
                 for c in range(BLOCKS):
                     nc.tensor.transpose(xt[:, c, :], words[:, c * P : (c + 1) * P], ident[:])
-                x_t[(i, n)] = xt
-            x_grouped[i] = grouped
+                x_t[PAIR * pair + n] = xt
 
-        def regroup(i, n):
+        def regroup(t):
+            if not is_tile(t):
+                return
             nc.scalar.copy(
-                out=x_grouped[i][:, n].bitcast(F32),
-                in_=x_t[(i, n)][:].rearrange("p (g u) t -> p g t u", u=2),
+                out=x_grouped[t // PAIR][:, t % PAIR].bitcast(F32),
+                in_=x_t[t][:].rearrange("p (g u) r -> p g r u", u=2),
             )
 
-        def quantise_pair(i):
-            codes = code_pool.tile([P, PAIR, PASSES, P], U32, align_bytes=64, name="x_codes")
-            scales = code_pool.tile([P, PAIR, PASSES, P], U8, align_bytes=64, name="x_scales")
+        def quantise_pair(pair):
+            if not is_pair(pair):
+                return
+            stream, m = tiles[PAIR * pair]
+            if m == 0:
+                quantise_weights(stream)
+            codes = ring3.tile([P, PAIR, PASSES, P], U32, align_bytes=64, name="x_codes")
+            scales = ring3.tile([P, PAIR, PASSES, P], U8, align_bytes=64, name="x_scales")
             nc.vector.quantize_mx(
-                out=codes[:].rearrange("p n g t -> p (n g t)").bitcast(FP8X4),
-                scales=scales[:].rearrange("p n g t -> p (n g t)"),
-                in_=x_grouped[i][:].rearrange("p n g t j -> p (n g t j)"),
+                out=codes[:].rearrange("p n g r -> p (n g r)").bitcast(FP8X4),
+                scales=scales[:].rearrange("p n g r -> p (n g r)"),
+                in_=x_grouped[pair][:].rearrange("p n g r j -> p (n g r j)"),
             )
-            x_codes[i] = codes
-            x_scales[i] = scales
+            x_codes[pair] = codes
+            x_scales[pair] = scales
 
-        def make_tables(i):
-            stream, m = pairs[i]
+        def project_pair(pair):
+            if not is_pair(pair):
+                return
+            stream = tiles[PAIR * pair][0]
             for n in range(PAIR):
-                tab = table_pool.tile([P, 2, 2, 2, HALF], F32, name="tab")
-                for cs, name, gain in ((0, "cos", gain_cos), (1, "sin", gain_sin)):
-                    planes = trig[(name, stream)][:, m + n, :].rearrange("p (i two) -> p two i", two=2)
-                    nc.gpsimd.tensor_tensor(
-                        out=tab[:, cs],
-                        in0=planes.unsqueeze(1).to_broadcast([P, 2, 2, HALF]),
-                        in1=gain[stream][:],
-                        op=ALU.mult,
-                    )
-                tables[(i, n)] = tab
-
-        def project_pair(i):
-            stream = pairs[i][0]
-            for n in range(PAIR):
-                y = psum_y.tile([P, 4, HEAD], F32, tag="y")
+                acc = psum_y.tile([P, OUTS], F32, tag="y")
                 for g in range(PASSES):
                     nc.tensor.matmul_mx(
-                        out=y[:].rearrange("p v c -> p (v c)"),
-                        lhsT=x_codes[i][:, n, g, :].bitcast(FP8X4),
-                        lhsT_scale=x_scales[i][:, n, g, :],
+                        out=acc[:],
+                        lhsT=x_codes[pair][:, n, g, :].bitcast(FP8X4),
+                        lhsT_scale=x_scales[pair][:, n, g, :],
                         rhs=w_codes[stream][:, g, :].bitcast(FP8X4),
                         rhs_scale=w_scales[stream][:, g, :],
                         start=(g == 0),
                         stop=(g == PASSES - 1),
                     )
-                y_ps[(i, n)] = y
+                y[PAIR * pair + n] = acc
 
-        rstd = {}
-
-        def add_bias(i, n):
-            if pairs[i][0] == TXT:
-                yb = work.tile([P, 4, HEAD], F32, name="yb")
-                nc.vector.tensor_tensor(
-                    out=yb[:], in0=y_ps[(i, n)][:], in1=bias[:].rearrange("p v two i -> p v (two i)"), op=ALU.add
-                )
-                y_ps[(i, n)] = yb
-
-        def inverse_rms(i, n):
-            y = y_ps[(i, n)]
-            squares = work.tile([P, 4, HEAD], BF16, name="squares")
-            sumsq = work.tile([P, 4], F32, name="sumsq")
-            for v in range(4):
-                nc.scalar.activation(
-                    out=squares[:, v, :], in_=y[:, v, :], func=ACT.Square, accum_out=sumsq[:, v : v + 1]
-                )
-            r = work.tile([P, 4], F32, name="r")
-            nc.scalar.activation(out=r[:], in_=sumsq[:], func=ACT.Abs_reciprocal_sqrt, bias=EPS, scale=1.0 / HEAD)
-            rstd[(i, n)] = r
-
-        rotated = {}
-
-        def rotate(i, n):
-            tab = tables[(i, n)]
-            y4 = y_ps[(i, n)][:].rearrange("p (q h) c -> p q h c", q=2)
-            straight = work.tile([P, 2, 2, HEAD], F32, name="straight")
+        def make_table(t):
+            if not is_tile(t):
+                return
+            stream, m = tiles[t]
+            tab = table_pool.tile([P, 2, 2, 2, HALF], F32, name="tab")
+            planes = trig[stream][:, m].rearrange("p cs j -> p (cs j)").rearrange("p (ci two) -> p two ci", two=2)
             nc.vector.tensor_tensor(
-                out=straight[:],
-                in0=y4,
-                in1=tab[:, 0].rearrange("p q two i -> p q (two i)").unsqueeze(2).to_broadcast([P, 2, 2, HEAD]),
+                out=tab[:].rearrange("p q two cs i -> p q two (cs i)"),
+                in0=planes.unsqueeze(1).to_broadcast([P, 2, 2, HEAD]),
+                in1=gains[:, stream, :].rearrange("p (q two c) -> p q two c", q=2, two=2),
                 op=ALU.mult,
             )
-            crossed = work.tile([P, 2, 2, HEAD], F32, name="crossed")
+            table[t] = tab
+
+        def add_bias(t):
+            if not is_tile(t) or tiles[t][0] != TXT:
+                return
+            biased = ring4.tile([P, OUTS], F32, name="biased")
+            nc.vector.tensor_tensor(out=biased[:], in0=y[t][:], in1=bias[:], op=ALU.add)
+            y[t] = biased
+
+        def by_plane(ap):
+            return ap.rearrange("p (q two h i) -> p q two h i", q=2, two=2, h=2)
+
+        def sum_squares(t):
+            if not is_tile(t):
+                return
+            squares = ring3.tile([P, OUTS], BF16, name="squares")
+            sums = ring6.tile([P, 4], F32, name="sums")
+            for q in range(2):
+                for h in range(2):
+                    nc.scalar.activation(
+                        out=by_plane(squares[:])[:, q, :, h, :],
+                        in_=by_plane(y[t][:])[:, q, :, h, :],
+                        func=ACT.Square,
+                        accum_out=sums[:, 2 * q + h : 2 * q + h + 1],
+                    )
+            rstd_in[t] = sums
+
+        def inverse_rms(t):
+            if not is_tile(t):
+                return
+            r = ring6.tile([P, 4], F32, name="r")
+            nc.scalar.activation(out=r[:], in_=rstd_in[t][:], func=ACT.Abs_reciprocal_sqrt, bias=EPS, scale=1.0 / HEAD)
+            rstd[t] = r
+
+        def multiply(t):
+            if not is_tile(t):
+                return
+            tab = table[t]
+            a = ring3.tile([P, OUTS], F32, name="a")
+            nc.vector.tensor_tensor(
+                out=a[:].rearrange("p (v h i) -> p v h i", v=4, h=2),
+                in0=y[t][:].rearrange("p (v h i) -> p v h i", v=4, h=2),
+                in1=tab[:, :, :, 0, :].rearrange("p q two i -> p (q two) i").unsqueeze(2).to_broadcast([P, 4, 2, HALF]),
+                op=ALU.mult,
+            )
+            b = ring3.tile([P, OUTS], F32, name="b")
             for two in range(2):
-                here = slice(two * HALF, (two + 1) * HALF)
-                there = slice((1 - two) * HALF, (2 - two) * HALF)
                 nc.vector.tensor_tensor(
-                    out=crossed[:, :, :, here],
-                    in0=y4[:, :, :, there],
-                    in1=tab[:, 1, :, two, :].unsqueeze(2).to_broadcast([P, 2, 2, HALF]),
+                    out=by_plane(b[:])[:, :, two],
+                    in0=by_plane(y[t][:])[:, :, 1 - two],
+                    in1=tab[:, :, two, 1, :].unsqueeze(2).to_broadcast([P, 2, 2, HALF]),
                     op=ALU.mult,
                 )
-            rot = work.tile([P, 4, HEAD], F32, name="rot")
-            nc.vector.tensor_tensor(
-                out=rot[:].rearrange("p (q h) c -> p q h c", q=2), in0=straight[:], in1=crossed[:], op=ALU.add
-            )
-            rotated[(i, n)] = rot
+            straight[t] = a
+            crossed[t] = b
 
-        def scale_and_store(i, n):
-            stream, m = pairs[i]
-            result = out_pool.tile([P, 4, HEAD], F32, name="result")
-            for v in range(4):
-                nc.scalar.activation(
-                    out=result[:, v, :].rearrange("p (i two) -> p i two", two=2),
-                    in_=rotated[(i, n)][:, v, :].rearrange("p (two i) -> p i two", two=2),
-                    func=ACT.Copy,
-                    scale=rstd[(i, n)][:, v : v + 1],
-                )
-            nc.sync.dma_start(out=q_dram[stream][:, m + n, :], in_=result[:, 0:2, :].rearrange("p h c -> p (h c)"))
-            nc.sync.dma_start(out=k_dram[stream][:, m + n, :], in_=result[:, 2:4, :].rearrange("p h c -> p (h c)"))
+        def add(t):
+            if not is_tile(t):
+                return
+            rot = ring3.tile([P, OUTS], F32, name="rot")
+            nc.gpsimd.tensor_tensor(out=rot[:], in0=straight[t][:], in1=crossed[t][:], op=ALU.add)
+            rotated[t] = rot
 
-        tiles = [(i, n) for i in range(len(pairs)) for n in range(PAIR)]
-        for step in range(-AHEAD, len(pairs)):
-            ahead = step + AHEAD
-            if ahead < len(pairs):
-                if pairs[ahead][1] == 0:
-                    prepare_weights(pairs[ahead][0])
-                transpose_pair(ahead)
-                make_tables(ahead)
-            if 0 <= step + 1 < len(pairs):
-                project_pair(step + 1)
-            if step == -1:
-                add_bias(0, 0)
-                inverse_rms(0, 0)
-            for n in range(PAIR):
-                if step >= 0:
-                    t = PAIR * step + n
-                    if t + 1 < len(tiles):
-                        add_bias(*tiles[t + 1])
-                        inverse_rms(*tiles[t + 1])
-                    rotate(step, n)
-                if ahead < len(pairs):
-                    regroup(ahead, n)
-                if step >= 0:
-                    scale_and_store(step, n)
-            if ahead < len(pairs):
-                quantise_pair(ahead)
+        def scale_and_store(t):
+            if not is_tile(t):
+                return
+            stream, m = tiles[t]
+            result = ring4.tile([P, 2, 2, HEAD], F32, name="result")
+            for q in range(2):
+                for h in range(2):
+                    nc.scalar.activation(
+                        out=result[:, q, h, :].rearrange("p (i two) -> p i two", two=2),
+                        in_=by_plane(rotated[t][:])[:, q, :, h, :].rearrange("p two i -> p i two"),
+                        func=ACT.Copy,
+                        scale=rstd[t][:, 2 * q + h : 2 * q + h + 1],
+                    )
+            nc.sync.dma_start(out=q_dram[stream][:, m, :], in_=result[:, 0].rearrange("p h c -> p (h c)"))
+            nc.sync.dma_start(out=k_dram[stream][:, m, :], in_=result[:, 1].rearrange("p h c -> p (h c)"))
+
+        W_LEAD = 8
+        TABLE_LEAD = 4
+        with tc.manual_schedule():
+            for t in range(n_tiles[TXT]):
+                make_table(t)
+            for t in range(-W_LEAD, len(tiles) + 2):
+                pair = t // PAIR
+                if t % PAIR == 0:
+                    project_pair(pair + 1)
+                for stream in (TXT, IMG):
+                    plane = t - (first_tile[stream] - W_LEAD)
+                    if 0 <= plane < 4:
+                        transpose_weight_plane(stream, plane)
+                if t % PAIR == 0:
+                    transpose_pair(pair + 3)
+                    quantise_pair(pair + 2)
+                sum_squares(t + 1)
+                if t + TABLE_LEAD >= n_tiles[TXT]:
+                    make_table(t + TABLE_LEAD)
+                multiply(t)
+                add_bias(t + 2)
+                regroup(t + 6)
+                inverse_rms(t + 1)
+                add(t - 1)
+                scale_and_store(t - 2)

@@ -347,14 +347,13 @@ def tile_flux2attention_pa_t_kernel(
                 make_table(t)
             for t in range(-W_LEAD, len(tiles) + 2):
                 pair = t // PAIR
-                if t % PAIR == 0:
-                    project_pair(pair + 1)
                 for stream in (TXT, IMG):
                     plane = t - (first_tile[stream] - W_LEAD)
                     if 0 <= plane < 4:
                         transpose_weight_plane(stream, plane)
                 if t % PAIR == 0:
                     transpose_pair(pair + 3)
+                    project_pair(pair + 1)
                     quantise_pair(pair + 2)
                 sum_squares(t + 1)
                 if t + TABLE_LEAD >= n_tiles[TXT]:

@@ -147,6 +147,8 @@ def tile_flux2attention_pa_t_kernel(
         gains = psum_g.tile([P, 2, OUTS], BF16)
         for stream in (TXT, IMG):
             nc.tensor.matmul(out=gains[:, stream, :], lhsT=ones[:], rhs=ordered[:, stream, :], start=True, stop=True)
+        gains_sb = const.tile([P, 2, OUTS], BF16)
+        nc.vector.tensor_copy(out=gains_sb[:], in_=gains[:])
         bias_ps = psum_y.tile([P, OUTS], F32, tag="y")
         nc.tensor.matmul(out=bias_ps[:], lhsT=ones[:], rhs=ordered[:, 2, :], start=True, stop=True)
         bias = const.tile([P, OUTS], F32)
@@ -255,10 +257,11 @@ def tile_flux2attention_pa_t_kernel(
             stream, m = tiles[t]
             tab = table_pool.tile([P, 2, 2, 2, HALF], F32, name="tab")
             planes = trig[stream][:, m].rearrange("p cs j -> p (cs j)").rearrange("p (ci two) -> p two ci", two=2)
-            nc.vector.tensor_tensor(
+            engine, factors = (nc.vector, gains) if t % 2 == 0 else (nc.gpsimd, gains_sb)
+            engine.tensor_tensor(
                 out=tab[:].rearrange("p q two cs i -> p q two (cs i)"),
                 in0=planes.unsqueeze(1).to_broadcast([P, 2, 2, HEAD]),
-                in1=gains[:, stream, :].rearrange("p (q two c) -> p q two c", q=2, two=2),
+                in1=factors[:, stream, :].rearrange("p (q two c) -> p q two c", q=2, two=2),
                 op=ALU.mult,
             )
             table[t] = tab
@@ -356,11 +359,11 @@ def tile_flux2attention_pa_t_kernel(
                     project_pair(pair + 1)
                     quantise_pair(pair + 2)
                 sum_squares(t + 1)
+                add(t - 1)
                 if t + TABLE_LEAD >= n_tiles[TXT]:
                     make_table(t + TABLE_LEAD)
                 multiply(t)
                 add_bias(t + 2)
                 regroup(t + 6)
                 inverse_rms(t + 1)
-                add(t - 1)
                 scale_and_store(t - 2)

@@ -18,10 +18,23 @@ BLOCKS = 4
 HEAD = 128
 HALF = 64
 OUTS = 512
+PLANES = 4
 S_TXT = 1024
 S_IMG = 3072
 EPS = 1e-5
 PAIR = 2
+RUN = 2
+
+WEIGHTS_AHEAD = 8
+TRANSPOSE_AHEAD = 5
+PROJECT_AHEAD = 2
+TRIG_CHUNK = 8
+TABLE_AHEAD = TRIG_CHUNK
+TEXT_TABLE_AHEAD = 1
+BIAS_AHEAD = 1
+NORM_AHEAD = 1
+ADD_BEHIND = 1
+STORE_BEHIND = 2
 
 FLOPS = 2 * (S_TXT + S_IMG) * K * OUTS
 
@@ -49,12 +62,12 @@ def tile_flux2attention_pa_t_kernel(
     TXT, IMG = 0, 1
     first_row = (0, S_TXT)
     n_tiles = (S_TXT // P, S_IMG // P)
-    first_tile = (0, S_TXT // P)
+    first_tile = (S_IMG // P, 0)
     weights = ((Waq, Wak), (Wq, Wk))
 
-    def by_partition(table, stream):
+    def by_partition(rows, stream):
         lo = first_row[stream]
-        return table[lo : lo + n_tiles[stream] * P, :].rearrange("(p m) c -> p m c", p=P)
+        return rows[lo : lo + n_tiles[stream] * P, :].rearrange("(p m) c -> p m c", p=P)
 
     x_dram = (
         encoder_hidden_states.rearrange("b (p m) k -> p (b m) k", p=P),
@@ -65,27 +78,29 @@ def tile_flux2attention_pa_t_kernel(
     q_dram = (by_partition(q_rows, TXT), by_partition(q_rows, IMG))
     k_dram = (by_partition(k_rows, TXT), by_partition(k_rows, IMG))
 
-    tiles = [(s, m) for s in (TXT, IMG) for m in range(n_tiles[s])]
+    tiles = [(s, m) for s in (IMG, TXT) for m in range(n_tiles[s])]
     n_pairs = len(tiles) // PAIR
 
     with ExitStack() as ctx:
         const = ctx.enter_context(tc.tile_pool(name="const", bufs=1))
         x_pool = ctx.enter_context(tc.tile_pool(name="x_pool", bufs=n_pairs))
-        w_pool = ctx.enter_context(tc.tile_pool(name="w_pool", bufs=8))
+        w_pool = ctx.enter_context(tc.tile_pool(name="w_pool", bufs=4))
         ring3 = ctx.enter_context(tc.tile_pool(name="ring3", bufs=3))
         ring4 = ctx.enter_context(tc.tile_pool(name="ring4", bufs=4))
         ring6 = ctx.enter_context(tc.tile_pool(name="ring6", bufs=6))
-        table_pool = ctx.enter_context(tc.tile_pool(name="table_pool", bufs=S_TXT // P + 1))
+        out_pool = ctx.enter_context(tc.tile_pool(name="out_pool", bufs=8))
+        table_pool = ctx.enter_context(tc.tile_pool(name="table_pool", bufs=TABLE_AHEAD + 1))
         psum_g = ctx.enter_context(tc.psum_pool(name="psum_g", bufs=1))
         psum_t = ctx.enter_context(tc.psum_pool(name="psum_t", bufs=3))
         psum_y = ctx.enter_context(tc.psum_pool(name="psum_y", bufs=4))
 
         vectors = const.tile([1, 2 * OUTS], BF16)
-        col = 0
-        for vec in (waq_norm, wak_norm, wq_norm, wk_norm, baq, bak):
-            n = vec.shape[0]
-            nc.scalar.dma_start(out=vectors[:, col : col + n], in_=vec.unsqueeze(0))
-            col += n
+
+        def load_vectors(vecs, col):
+            for vec in vecs:
+                n = vec.shape[0]
+                nc.sync.dma_start(out=vectors[:, col : col + n], in_=vec.unsqueeze(0))
+                col += n
 
         w_raw = {}
         x_raw = {}
@@ -93,44 +108,59 @@ def tile_flux2attention_pa_t_kernel(
 
         def load_weights(stream):
             for qk in range(2):
-                by_parity = weights[stream][qk].rearrange("(hi two) k -> two hi k", two=2)
+                rows = w_pool.tile([P, 2, K], BF16, name="w_raw%d%d" % (stream, qk), tag="w_raw")
+                nc.sync.dma_start(out=rows[:], in_=weights[stream][qk].rearrange("(hi two) k -> hi two k", two=2))
                 for two in range(2):
-                    t = w_pool.tile([P, K], BF16, name="w_raw%d%d%d" % (stream, qk, two), tag="w_raw")
-                    nc.sync.dma_start(out=t[:], in_=by_parity[two])
-                    w_raw[(stream, 2 * qk + two)] = t
+                    w_raw[(stream, 2 * qk + two)] = rows[:, two, :]
 
         def load_pair(pair):
             stream, m = tiles[PAIR * pair]
-            t = x_pool.tile([P, PAIR, K], BF16, name="x_raw%d" % pair, tag="x_raw")
-            nc.sync.dma_start(out=t[:], in_=x_dram[stream][:, m : m + PAIR, :])
-            x_raw[pair] = t
+            rows = x_pool.tile([P, PAIR, K], BF16, name="x_raw%d" % pair, tag="x_raw")
+            nc.sync.dma_start(out=rows[:], in_=x_dram[stream][:, m : m + PAIR, :])
+            x_raw[pair] = rows
 
-        def load_trig(stream):
-            t = const.tile([P, n_tiles[stream], 2, HEAD], BF16, name="trig%d" % stream)
-            nc.sync.dma_start(out=t[:, :, 0, :], in_=by_partition(rope_cos, stream))
-            nc.sync.dma_start(out=t[:, :, 1, :], in_=by_partition(rope_sin, stream))
-            trig[stream] = t
+        def load_trig(chunk):
+            stream, m = tiles[chunk * TRIG_CHUNK]
+            both = const.tile([P, TRIG_CHUNK, 2, HEAD], BF16, name="trig%d" % chunk)
+            nc.sync.dma_start(out=both[:, :, 0, :], in_=by_partition(rope_cos, stream)[:, m : m + TRIG_CHUNK, :])
+            nc.sync.dma_start(out=both[:, :, 1, :], in_=by_partition(rope_sin, stream)[:, m : m + TRIG_CHUNK, :])
+            trig[chunk] = both
 
-        load_trig(TXT)
-        load_weights(TXT)
-        load_pair(0)
-        load_pair(1)
-        load_pair(2)
-        load_pair(3)
+        load_vectors((wq_norm, wk_norm), 2 * HEAD)
+        load_trig(0)
         load_weights(IMG)
-        load_pair(4)
-        load_trig(IMG)
-        for pair in range(5, n_pairs):
+        for pair in range(0, 2):
+            load_pair(pair)
+        load_vectors((waq_norm, wak_norm), 0)
+        load_vectors((baq, bak), OUTS)
+        for pair in range(2, 4):
+            load_pair(pair)
+        load_trig(1)
+        for pair in range(4, 7):
+            load_pair(pair)
+        load_trig(2)
+        for pair in range(7, 10):
+            load_pair(pair)
+        load_weights(TXT)
+        load_trig(3)
+        for pair in range(10, n_pairs):
             load_pair(pair)
 
         ident = const.tile([P, P], F32)
         make_identity(nc, ident[:])
+        ident_bf = const.tile([P, P], BF16)
+        make_identity(nc, ident_bf[:])
 
         ones = const.tile([P, P], BF16)
         nc.vector.memset(ones[:], 1.0)
         ordered = const.tile([P, 3, OUTS], BF16)
         nc.vector.memset(ordered[:], 0.0)
-        for stream in (TXT, IMG):
+        gains = psum_g.tile([P, 2, OUTS], BF16)
+        bias = const.tile([P, OUTS], F32)
+        diagonal = const.tile([P, 2, OUTS], BF16)
+        nc.vector.memset(diagonal[:], 0.0)
+
+        def order_gains(stream):
             w = vectors[:, 2 * HEAD * stream : 2 * HEAD * (stream + 1)].rearrange(
                 "p (q i two) -> p q two i", q=2, two=2
             )
@@ -138,23 +168,48 @@ def tile_flux2attention_pa_t_kernel(
             nc.vector.tensor_copy(out=g[:, :, :, 0, :], in_=w)
             nc.vector.tensor_scalar_mul(out=g[:, :, 0, 1, :], in0=w[:, :, 1, :], scalar1=-1.0)
             nc.vector.tensor_copy(out=g[:, :, 1, 1, :], in_=w[:, :, 0, :])
-        for qk in range(2):
-            lo = qk * 2 * HEAD
-            nc.vector.tensor_copy(
-                out=ordered[0:1, 2, lo : lo + 2 * HEAD].rearrange("p (two h i) -> p two h i", two=2, h=2),
-                in_=vectors[:, OUTS + lo : OUTS + lo + 2 * HEAD].rearrange("p (h i two) -> p two h i", h=2, two=2),
-            )
-        gains = psum_g.tile([P, 2, OUTS], BF16)
-        for stream in (TXT, IMG):
+
+        def spread_gains(stream):
             nc.tensor.matmul(out=gains[:, stream, :], lhsT=ones[:], rhs=ordered[:, stream, :], start=True, stop=True)
-        gains_sb = const.tile([P, 2, OUTS], BF16)
-        nc.vector.tensor_copy(out=gains_sb[:], in_=gains[:])
-        bias_ps = psum_y.tile([P, OUTS], F32, tag="y")
-        nc.tensor.matmul(out=bias_ps[:], lhsT=ones[:], rhs=ordered[:, 2, :], start=True, stop=True)
-        bias = const.tile([P, OUTS], F32)
-        nc.vector.tensor_copy(out=bias[:], in_=bias_ps[:])
+
+        def order_bias():
+            for qk in range(2):
+                lo = qk * 2 * HEAD
+                nc.vector.tensor_copy(
+                    out=ordered[0:1, 2, lo : lo + 2 * HEAD].rearrange("p (two h i) -> p two h i", two=2, h=2),
+                    in_=vectors[:, OUTS + lo : OUTS + lo + 2 * HEAD].rearrange("p (h i two) -> p two h i", h=2, two=2),
+                )
+
+        def spread_bias():
+            bias_ps = psum_t.tile([P, OUTS], F32, tag="t")
+            nc.tensor.matmul(out=bias_ps[:], lhsT=ones[:], rhs=ordered[:, 2, :], start=True, stop=True)
+            return bias_ps
+
+        def gains_on_diagonal():
+            hit = ident_bf[:].rearrange("p (i two) -> p two i", two=2)
+            for cs in range(2):
+                nc.vector.tensor_tensor(
+                    out=diagonal[:, cs, :].rearrange("p (q two cs i) -> p q two cs i", q=2, two=2, cs=2)[:, :, :, cs, :],
+                    in0=gains[:, TXT, :].rearrange("p (q two cs i) -> p q two cs i", q=2, two=2, cs=2)[:, :, :, cs, :],
+                    in1=hit.unsqueeze(1).to_broadcast([P, 2, 2, HALF]),
+                    op=ALU.mult,
+                )
+
+        trig_t = {}
+
+        def transpose_trig(cs):
+            both = trig[first_tile[TXT] // TRIG_CHUNK]
+            bank = psum_t.tile([P, TRIG_CHUNK, P], BF16, tag="t")
+            for m in range(TRIG_CHUNK):
+                nc.tensor.transpose(bank[:, m, :], both[:, m, cs, :], ident_bf[:])
+            return bank
+
+        def keep_trig(cs, bank):
+            trig_t[cs] = const.tile([P, TRIG_CHUNK, P], BF16, name="trig_t%d" % cs)
+            nc.vector.tensor_copy(out=trig_t[cs][:], in_=bank[:])
 
         w_grouped = {}
+        w_t = {}
         w_codes = {}
         w_scales = {}
         x_t = {}
@@ -163,7 +218,7 @@ def tile_flux2attention_pa_t_kernel(
         x_scales = {}
         table = {}
         y = {}
-        rstd_in = {}
+        sumsq = {}
         rstd = {}
         straight = {}
         crossed = {}
@@ -178,13 +233,16 @@ def tile_flux2attention_pa_t_kernel(
         def transpose_weight_plane(stream, plane):
             if plane == 0:
                 w_grouped[stream] = const.tile([P, PASSES, OUTS, 4], BF16, align_bytes=64, name="w_grouped", tag="w_grouped")
-            words = w_raw[(stream, plane)][:].bitcast(F32)
+            words = w_raw[(stream, plane)].bitcast(F32)
             wt = psum_t.tile([P, BLOCKS, P], F32, tag="t")
             for c in range(BLOCKS):
                 nc.tensor.transpose(wt[:, c, :], words[:, c * P : (c + 1) * P], ident[:])
-            nc.scalar.copy(
+            w_t[(stream, plane)] = wt
+
+        def regroup_weight_plane(stream, plane, copy):
+            copy(
                 out=w_grouped[stream][:].bitcast(F32)[:, :, plane * P : (plane + 1) * P, :],
-                in_=wt[:].rearrange("p (g u) r -> p g r u", u=2),
+                in_=w_t[(stream, plane)][:].rearrange("p (g u) r -> p g r u", u=2),
             )
 
         def quantise_weights(stream):
@@ -198,16 +256,17 @@ def tile_flux2attention_pa_t_kernel(
             w_codes[stream] = codes
             w_scales[stream] = scales
 
-        def transpose_pair(pair):
-            if not is_pair(pair):
+        def transpose_tile(t):
+            if not is_tile(t):
                 return
-            x_grouped[pair] = ring3.tile([P, PAIR, PASSES, P, 4], BF16, align_bytes=64, name="x_grouped")
-            for n in range(PAIR):
-                words = x_raw[pair][:, n, :].bitcast(F32)
-                xt = psum_t.tile([P, BLOCKS, P], F32, tag="t")
-                for c in range(BLOCKS):
-                    nc.tensor.transpose(xt[:, c, :], words[:, c * P : (c + 1) * P], ident[:])
-                x_t[PAIR * pair + n] = xt
+            pair, n = divmod(t, PAIR)
+            if n == 0:
+                x_grouped[pair] = ring3.tile([P, PAIR, PASSES, P, 4], BF16, align_bytes=64, name="x_grouped")
+            words = x_raw[pair][:, n, :].bitcast(F32)
+            xt = psum_t.tile([P, BLOCKS, P], F32, tag="t")
+            for c in range(BLOCKS):
+                nc.tensor.transpose(xt[:, c, :], words[:, c * P : (c + 1) * P], ident[:])
+            x_t[t] = xt
 
         def regroup(t):
             if not is_tile(t):
@@ -233,37 +292,52 @@ def tile_flux2attention_pa_t_kernel(
             x_codes[pair] = codes
             x_scales[pair] = scales
 
-        def project_pair(pair):
-            if not is_pair(pair):
-                return
-            stream = tiles[PAIR * pair][0]
-            for n in range(PAIR):
-                acc = psum_y.tile([P, OUTS], F32, tag="y")
-                for g in range(PASSES):
-                    nc.tensor.matmul_mx(
-                        out=acc[:],
-                        lhsT=x_codes[pair][:, n, g, :].bitcast(FP8X4),
-                        lhsT_scale=x_scales[pair][:, n, g, :],
-                        rhs=w_codes[stream][:, g, :].bitcast(FP8X4),
-                        rhs_scale=w_scales[stream][:, g, :],
-                        start=(g == 0),
-                        stop=(g == PASSES - 1),
-                    )
-                y[PAIR * pair + n] = acc
-
-        def make_table(t):
+        def project_tile(t):
             if not is_tile(t):
                 return
-            stream, m = tiles[t]
+            stream = tiles[t][0]
+            pair, n = divmod(t, PAIR)
+            acc = psum_y.tile([P, OUTS], F32, tag="y")
+            for g in range(PASSES):
+                nc.tensor.matmul_mx(
+                    out=acc[:],
+                    lhsT=x_codes[pair][:, n, g, :].bitcast(FP8X4),
+                    lhsT_scale=x_scales[pair][:, n, g, :],
+                    rhs=w_codes[stream][:, g, :].bitcast(FP8X4),
+                    rhs_scale=w_scales[stream][:, g, :],
+                    start=(g == 0),
+                    stop=(g == PASSES - 1),
+                )
+            y[t] = acc
+
+        def make_table(t):
+            if not is_tile(t) or tiles[t][0] != IMG:
+                return
+            stream = tiles[t][0]
             tab = table_pool.tile([P, 2, 2, 2, HALF], F32, name="tab")
-            planes = trig[stream][:, m].rearrange("p cs j -> p (cs j)").rearrange("p (ci two) -> p two ci", two=2)
-            engine, factors = (nc.vector, gains) if t % 2 == 0 else (nc.gpsimd, gains_sb)
-            engine.tensor_tensor(
+            both = trig[t // TRIG_CHUNK][:, t % TRIG_CHUNK]
+            planes = both.rearrange("p cs j -> p (cs j)").rearrange("p (ci two) -> p two ci", two=2)
+            nc.vector.tensor_tensor(
                 out=tab[:].rearrange("p q two cs i -> p q two (cs i)"),
                 in0=planes.unsqueeze(1).to_broadcast([P, 2, 2, HEAD]),
-                in1=factors[:, stream, :].rearrange("p (q two c) -> p q two c", q=2, two=2),
+                in1=gains[:, stream, :].rearrange("p (q two c) -> p q two c", q=2, two=2),
                 op=ALU.mult,
             )
+            table[t] = tab
+
+        def project_table(t):
+            if not is_tile(t) or tiles[t][0] != TXT:
+                return
+            m = tiles[t][1]
+            tab = psum_y.tile([P, 2, 2, 2, HALF], F32, tag="y")
+            for cs in range(2):
+                nc.tensor.matmul(
+                    out=tab[:].rearrange("p q two cs i -> p (q two cs i)"),
+                    lhsT=trig_t[cs][:, m, :],
+                    rhs=diagonal[:, cs, :],
+                    start=(cs == 0),
+                    stop=(cs == 1),
+                )
             table[t] = tab
 
         def add_bias(t):
@@ -289,13 +363,13 @@ def tile_flux2attention_pa_t_kernel(
                         func=ACT.Square,
                         accum_out=sums[:, 2 * q + h : 2 * q + h + 1],
                     )
-            rstd_in[t] = sums
+            sumsq[t] = sums
 
         def inverse_rms(t):
             if not is_tile(t):
                 return
             r = ring6.tile([P, 4], F32, name="r")
-            nc.scalar.activation(out=r[:], in_=rstd_in[t][:], func=ACT.Abs_reciprocal_sqrt, bias=EPS, scale=1.0 / HEAD)
+            nc.scalar.activation(out=r[:], in_=sumsq[t][:], func=ACT.Abs_reciprocal_sqrt, bias=EPS, scale=1.0 / HEAD)
             rstd[t] = r
 
         def multiply(t):
@@ -304,9 +378,9 @@ def tile_flux2attention_pa_t_kernel(
             tab = table[t]
             a = ring3.tile([P, OUTS], F32, name="a")
             nc.vector.tensor_tensor(
-                out=a[:].rearrange("p (v h i) -> p v h i", v=4, h=2),
-                in0=y[t][:].rearrange("p (v h i) -> p v h i", v=4, h=2),
-                in1=tab[:, :, :, 0, :].rearrange("p q two i -> p (q two) i").unsqueeze(2).to_broadcast([P, 4, 2, HALF]),
+                out=a[:].rearrange("p (v h i) -> p v h i", v=PLANES, h=2),
+                in0=y[t][:].rearrange("p (v h i) -> p v h i", v=PLANES, h=2),
+                in1=tab[:, :, :, 0, :].rearrange("p q two i -> p (q two) i").unsqueeze(2).to_broadcast([P, PLANES, 2, HALF]),
                 op=ALU.mult,
             )
             b = ring3.tile([P, OUTS], F32, name="b")
@@ -320,18 +394,18 @@ def tile_flux2attention_pa_t_kernel(
             straight[t] = a
             crossed[t] = b
 
-        def add(t):
+        def add(t, engine):
             if not is_tile(t):
                 return
             rot = ring3.tile([P, OUTS], F32, name="rot")
-            nc.gpsimd.tensor_tensor(out=rot[:], in0=straight[t][:], in1=crossed[t][:], op=ALU.add)
+            engine.tensor_tensor(out=rot[:], in0=straight[t][:], in1=crossed[t][:], op=ALU.add)
             rotated[t] = rot
 
         def scale_and_store(t):
             if not is_tile(t):
                 return
             stream, m = tiles[t]
-            result = ring4.tile([P, 2, 2, HEAD], F32, name="result")
+            result = out_pool.tile([P, 2, 2, HEAD], F32, name="result")
             for q in range(2):
                 for h in range(2):
                     nc.scalar.activation(
@@ -343,27 +417,50 @@ def tile_flux2attention_pa_t_kernel(
             nc.sync.dma_start(out=q_dram[stream][:, m, :], in_=result[:, 0].rearrange("p h c -> p (h c)"))
             nc.sync.dma_start(out=k_dram[stream][:, m, :], in_=result[:, 1].rearrange("p h c -> p (h c)"))
 
-        W_LEAD = 8
-        TABLE_LEAD = 4
         with tc.manual_schedule():
-            for t in range(n_tiles[TXT]):
+            order_gains(IMG)
+            spread_gains(IMG)
+            for t in range(TABLE_AHEAD):
                 make_table(t)
-            for t in range(-W_LEAD, len(tiles) + 2):
-                pair = t // PAIR
-                for stream in (TXT, IMG):
-                    plane = t - (first_tile[stream] - W_LEAD)
-                    if 0 <= plane < 4:
-                        transpose_weight_plane(stream, plane)
-                if t % PAIR == 0:
-                    transpose_pair(pair + 3)
-                    project_pair(pair + 1)
-                    quantise_pair(pair + 2)
-                sum_squares(t + 1)
-                add(t - 1)
-                if t + TABLE_LEAD >= n_tiles[TXT]:
-                    make_table(t + TABLE_LEAD)
+            for t in range(-WEIGHTS_AHEAD, len(tiles) + STORE_BEHIND):
+                plane = t - (first_tile[IMG] - WEIGHTS_AHEAD)
+                if 0 <= plane < PLANES:
+                    transpose_weight_plane(IMG, plane)
+                    regroup_weight_plane(IMG, plane, nc.scalar.copy)
+                step = t - (first_tile[TXT] - WEIGHTS_AHEAD)
+                if 0 <= step < PLANES:
+                    transpose_weight_plane(TXT, step)
+                if t % RUN == RUN - 1:
+                    for n in range(RUN):
+                        transpose_tile(t + TRANSPOSE_AHEAD + n)
+                if t % RUN == 0:
+                    for n in range(RUN):
+                        project_tile(t + PROJECT_AHEAD + n)
+                if (t + 1 + PROJECT_AHEAD) % PAIR == 0:
+                    quantise_pair((t + 1 + PROJECT_AHEAD) // PAIR)
+                project_table(t + TEXT_TABLE_AHEAD)
+                if t == -PROJECT_AHEAD:
+                    order_gains(TXT)
+                    order_bias()
+                if step == 0:
+                    spread_gains(TXT)
+                    bias_ps = spread_bias()
+                if step == 1:
+                    nc.vector.tensor_copy(out=bias[:], in_=bias_ps[:])
+                    gains_on_diagonal()
+                if 1 <= step < PLANES + 1:
+                    regroup_weight_plane(TXT, step - 1, nc.vector.tensor_copy if step % 2 == 0 else nc.scalar.copy)
+                for cs in range(2):
+                    if step == PLANES + cs:
+                        trig_bank = transpose_trig(cs)
+                    if step == PLANES + cs + 1:
+                        keep_trig(cs, trig_bank)
+                add_bias(t + BIAS_AHEAD)
+                if t >= 0:
+                    make_table(t + TABLE_AHEAD)
                 multiply(t)
-                add_bias(t + 2)
-                regroup(t + 6)
-                inverse_rms(t + 1)
-                scale_and_store(t - 2)
+                add(t - ADD_BEHIND, nc.gpsimd if is_tile(t) else nc.vector)
+                regroup(t + TRANSPOSE_AHEAD)
+                sum_squares(t + NORM_AHEAD)
+                scale_and_store(t - STORE_BEHIND)
+                inverse_rms(t + NORM_AHEAD)

@@ -23,7 +23,7 @@ S_TXT = 1024
 S_IMG = 3072
 EPS = 1e-5
 PAIR = 2
-RUN = 2
+RUN = 1
 
 WEIGHTS_AHEAD = 8
 TRANSPOSE_AHEAD = 5

@@ -16,25 +16,27 @@ K = 1024
 PASSES = 2
 BLOCKS = 4
 HEAD = 128
-HALF = 64
 OUTS = 512
 PLANES = 4
 S_TXT = 1024
 S_IMG = 3072
 EPS = 1e-5
 PAIR = 2
-RUN = 1
+GROUP = 8
+TEXT_PLACES = (6, 7)
+LIFT_PLACES = (2, 3, 4, 5)
 
-WEIGHTS_AHEAD = 8
-TRANSPOSE_AHEAD = 5
-PROJECT_AHEAD = 2
-TRIG_CHUNK = 8
-TABLE_AHEAD = TRIG_CHUNK
-TEXT_TABLE_AHEAD = 1
-BIAS_AHEAD = 1
+IMG_WEIGHTS_AT = -11
+TXT_WEIGHTS_AT = -2
+TRANSPOSE_AHEAD = 7
+PROJECT_AHEAD = 3
+BIAS_AHEAD = 2
+SQUARES_AHEAD = 2
 NORM_AHEAD = 1
 ADD_BEHIND = 1
-STORE_BEHIND = 2
+TRIG_CHUNK = 8
+EARLY_TABLES = 4
+TABLE_AHEAD = 7
 
 FLOPS = 2 * (S_TXT + S_IMG) * K * OUTS
 
@@ -62,7 +64,6 @@ def tile_flux2attention_pa_t_kernel(
     TXT, IMG = 0, 1
     first_row = (0, S_TXT)
     n_tiles = (S_TXT // P, S_IMG // P)
-    first_tile = (S_IMG // P, 0)
     weights = ((Waq, Wak), (Wq, Wk))
 
     def by_partition(rows, stream):
@@ -78,8 +79,12 @@ def tile_flux2attention_pa_t_kernel(
     q_dram = (by_partition(q_rows, TXT), by_partition(q_rows, IMG))
     k_dram = (by_partition(k_rows, TXT), by_partition(k_rows, IMG))
 
-    tiles = [(s, m) for s in (IMG, TXT) for m in range(n_tiles[s])]
-    n_pairs = len(tiles) // PAIR
+    n_all = n_tiles[TXT] + n_tiles[IMG]
+    tiles = []
+    for t in range(n_all):
+        stream = TXT if t % GROUP in TEXT_PLACES else IMG
+        tiles.append((stream, len([s for s, m in tiles if s == stream])))
+    n_pairs = n_all // PAIR
 
     with ExitStack() as ctx:
         const = ctx.enter_context(tc.tile_pool(name="const", bufs=1))
@@ -89,10 +94,10 @@ def tile_flux2attention_pa_t_kernel(
         ring4 = ctx.enter_context(tc.tile_pool(name="ring4", bufs=4))
         ring6 = ctx.enter_context(tc.tile_pool(name="ring6", bufs=6))
         out_pool = ctx.enter_context(tc.tile_pool(name="out_pool", bufs=8))
-        table_pool = ctx.enter_context(tc.tile_pool(name="table_pool", bufs=TABLE_AHEAD + 1))
-        psum_g = ctx.enter_context(tc.psum_pool(name="psum_g", bufs=1))
-        psum_t = ctx.enter_context(tc.psum_pool(name="psum_t", bufs=3))
+        table_pool = ctx.enter_context(tc.tile_pool(name="table_pool", bufs=9))
+        psum_t = ctx.enter_context(tc.psum_pool(name="psum_t", bufs=2))
         psum_y = ctx.enter_context(tc.psum_pool(name="psum_y", bufs=4))
+        psum_x = ctx.enter_context(tc.psum_pool(name="psum_x", bufs=2))
 
         vectors = const.tile([1, 2 * OUTS], BF16)
 
@@ -109,43 +114,44 @@ def tile_flux2attention_pa_t_kernel(
         def load_weights(stream):
             for qk in range(2):
                 rows = w_pool.tile([P, 2, K], BF16, name="w_raw%d%d" % (stream, qk), tag="w_raw")
-                nc.sync.dma_start(out=rows[:], in_=weights[stream][qk].rearrange("(hi two) k -> hi two k", two=2))
-                for two in range(2):
-                    w_raw[(stream, 2 * qk + two)] = rows[:, two, :]
+                nc.sync.dma_start(out=rows[:], in_=weights[stream][qk].rearrange("(h d) k -> d h k", h=2))
+                for h in range(2):
+                    w_raw[(stream, 2 * qk + h)] = rows[:, h, :]
 
-        def load_pair(pair):
-            stream, m = tiles[PAIR * pair]
-            rows = x_pool.tile([P, PAIR, K], BF16, name="x_raw%d" % pair, tag="x_raw")
-            nc.sync.dma_start(out=rows[:], in_=x_dram[stream][:, m : m + PAIR, :])
-            x_raw[pair] = rows
+        def load_pairs(pairs):
+            for pair in pairs:
+                stream, m = tiles[PAIR * pair]
+                rows = x_pool.tile([P, PAIR, K], BF16, name="x_raw%d" % pair, tag="x_raw")
+                nc.sync.dma_start(out=rows[:], in_=x_dram[stream][:, m : m + PAIR, :])
+                x_raw[pair] = rows
 
-        def load_trig(chunk):
-            stream, m = tiles[chunk * TRIG_CHUNK]
-            both = const.tile([P, TRIG_CHUNK, 2, HEAD], BF16, name="trig%d" % chunk)
-            nc.sync.dma_start(out=both[:, :, 0, :], in_=by_partition(rope_cos, stream)[:, m : m + TRIG_CHUNK, :])
-            nc.sync.dma_start(out=both[:, :, 1, :], in_=by_partition(rope_sin, stream)[:, m : m + TRIG_CHUNK, :])
-            trig[chunk] = both
+        def load_trig(stream, chunk):
+            m = chunk * TRIG_CHUNK
+            both = const.tile([P, 2, TRIG_CHUNK, HEAD], BF16, name="trig%d%d" % (stream, chunk))
+            for cs, rows in enumerate((rope_cos, rope_sin)):
+                nc.sync.dma_start(out=both[:, cs], in_=by_partition(rows, stream)[:, m : m + TRIG_CHUNK, :])
+            for n in range(TRIG_CHUNK):
+                trig[(stream, m + n)] = both[:, :, n, :]
 
         load_vectors((wq_norm, wk_norm), 2 * HEAD)
-        load_trig(0)
+        load_trig(IMG, 0)
         load_weights(IMG)
-        for pair in range(0, 2):
-            load_pair(pair)
+        load_pairs(range(0, 2))
         load_vectors((waq_norm, wak_norm), 0)
         load_vectors((baq, bak), OUTS)
-        for pair in range(2, 4):
-            load_pair(pair)
-        load_trig(1)
-        for pair in range(4, 7):
-            load_pair(pair)
-        load_trig(2)
-        for pair in range(7, 10):
-            load_pair(pair)
+        load_pairs(range(2, 3))
         load_weights(TXT)
-        load_trig(3)
-        for pair in range(10, n_pairs):
-            load_pair(pair)
+        load_pairs(range(3, 4))
+        load_trig(TXT, 0)
+        load_trig(IMG, 1)
+        load_pairs(range(4, 8))
+        load_trig(IMG, 2)
+        load_pairs(range(8, n_pairs))
 
+        one = const.tile([P, 1], F32)
+        nc.vector.memset(one[:], 1.0)
+        warm = const.tile([P, 1], F32)
+        nc.scalar.activation(out=warm[:], in_=one[:], func=ACT.Abs_reciprocal_sqrt, bias=EPS, scale=1.0 / HEAD)
         ident = const.tile([P, P], F32)
         make_identity(nc, ident[:])
         ident_bf = const.tile([P, P], BF16)
@@ -155,58 +161,37 @@ def tile_flux2attention_pa_t_kernel(
         nc.vector.memset(ones[:], 1.0)
         ordered = const.tile([P, 3, OUTS], BF16)
         nc.vector.memset(ordered[:], 0.0)
-        gains = psum_g.tile([P, 2, OUTS], BF16)
+        gains = const.tile([P, 2, OUTS], BF16)
         bias = const.tile([P, OUTS], F32)
-        diagonal = const.tile([P, 2, OUTS], BF16)
-        nc.vector.memset(diagonal[:], 0.0)
+        diagonal = {s: const.tile([P, 2, 2, HEAD], BF16, name="diagonal%d" % s) for s in (IMG, TXT)}
 
         def order_gains(stream):
-            w = vectors[:, 2 * HEAD * stream : 2 * HEAD * (stream + 1)].rearrange(
-                "p (q i two) -> p q two i", q=2, two=2
-            )
-            g = ordered[0:1, stream, :].rearrange("p (q two cs i) -> p q two cs i", q=2, two=2, cs=2)
-            nc.vector.tensor_copy(out=g[:, :, :, 0, :], in_=w)
-            nc.vector.tensor_scalar_mul(out=g[:, :, 0, 1, :], in0=w[:, :, 1, :], scalar1=-1.0)
-            nc.vector.tensor_copy(out=g[:, :, 1, 1, :], in_=w[:, :, 0, :])
-
-        def spread_gains(stream):
-            nc.tensor.matmul(out=gains[:, stream, :], lhsT=ones[:], rhs=ordered[:, stream, :], start=True, stop=True)
+            w = vectors[:, 2 * HEAD * stream : 2 * HEAD * (stream + 1)]
+            g = ordered[0:1, stream, :].rearrange("p (cs c) -> p cs c", cs=2)
+            pairs = w.rearrange("p (ci two) -> p ci two", two=2)
+            beside_sin = g[:, 1, :].rearrange("p (ci two) -> p ci two", two=2)
+            nc.vector.tensor_copy(out=g[:, 0, :], in_=w)
+            nc.vector.tensor_scalar_mul(out=beside_sin[:, :, 0], in0=pairs[:, :, 1], scalar1=-1.0)
+            nc.vector.tensor_copy(out=beside_sin[:, :, 1], in_=pairs[:, :, 0])
 
         def order_bias():
-            for qk in range(2):
-                lo = qk * 2 * HEAD
-                nc.vector.tensor_copy(
-                    out=ordered[0:1, 2, lo : lo + 2 * HEAD].rearrange("p (two h i) -> p two h i", two=2, h=2),
-                    in_=vectors[:, OUTS + lo : OUTS + lo + 2 * HEAD].rearrange("p (h i two) -> p two h i", h=2, two=2),
-                )
+            nc.vector.tensor_copy(out=ordered[0:1, 2, :], in_=vectors[:, OUTS : 2 * OUTS])
 
-        def spread_bias():
-            bias_ps = psum_t.tile([P, OUTS], F32, tag="t")
-            nc.tensor.matmul(out=bias_ps[:], lhsT=ones[:], rhs=ordered[:, 2, :], start=True, stop=True)
-            return bias_ps
-
-        def gains_on_diagonal():
-            hit = ident_bf[:].rearrange("p (i two) -> p two i", two=2)
-            for cs in range(2):
-                nc.vector.tensor_tensor(
-                    out=diagonal[:, cs, :].rearrange("p (q two cs i) -> p q two cs i", q=2, two=2, cs=2)[:, :, :, cs, :],
-                    in0=gains[:, TXT, :].rearrange("p (q two cs i) -> p q two cs i", q=2, two=2, cs=2)[:, :, :, cs, :],
-                    in1=hit.unsqueeze(1).to_broadcast([P, 2, 2, HALF]),
-                    op=ALU.mult,
-                )
-
-        trig_t = {}
-
-        def transpose_trig(cs):
-            both = trig[first_tile[TXT] // TRIG_CHUNK]
-            bank = psum_t.tile([P, TRIG_CHUNK, P], BF16, tag="t")
-            for m in range(TRIG_CHUNK):
-                nc.tensor.transpose(bank[:, m, :], both[:, m, cs, :], ident_bf[:])
+        def spread(row):
+            bank = psum_x.tile([P, OUTS], F32, name="spread%d" % row, tag="x")
+            nc.tensor.matmul(out=bank[:], lhsT=ones[:], rhs=ordered[:, row, :], start=True, stop=True)
             return bank
 
-        def keep_trig(cs, bank):
-            trig_t[cs] = const.tile([P, TRIG_CHUNK, P], BF16, name="trig_t%d" % cs)
-            nc.vector.tensor_copy(out=trig_t[cs][:], in_=bank[:])
+        def keep_gains(stream, bank):
+            nc.vector.tensor_copy(out=gains[:, stream, :], in_=bank[:])
+
+        def gains_on_diagonal(stream):
+            nc.vector.tensor_tensor(
+                out=diagonal[stream][:],
+                in0=gains[:, stream, :].rearrange("p (cs q d) -> p cs q d", cs=2, q=2),
+                in1=ident_bf[:].unsqueeze(1).unsqueeze(1).to_broadcast([P, 2, 2, HEAD]),
+                op=ALU.mult,
+            )
 
         w_grouped = {}
         w_t = {}
@@ -216,25 +201,31 @@ def tile_flux2attention_pa_t_kernel(
         x_grouped = {}
         x_codes = {}
         x_scales = {}
+        trig_t = {}
         table = {}
         y = {}
         sumsq = {}
         rstd = {}
         straight = {}
         crossed = {}
-        rotated = {}
 
         def is_tile(t):
-            return 0 <= t < len(tiles)
+            return 0 <= t < n_all
 
-        def is_pair(pair):
-            return 0 <= pair < n_pairs
+        def is_text(t):
+            return is_tile(t) and tiles[t][0] == TXT
+
+        def is_lifted(t):
+            return GROUP <= t < n_all and t % GROUP in LIFT_PLACES
 
         def transpose_weight_plane(stream, plane):
             if plane == 0:
-                w_grouped[stream] = const.tile([P, PASSES, OUTS, 4], BF16, align_bytes=64, name="w_grouped", tag="w_grouped")
+                w_grouped[stream] = const.tile([P, PASSES, OUTS, 4], BF16, align_bytes=64, name="w_grouped%d" % stream)
             words = w_raw[(stream, plane)].bitcast(F32)
-            wt = psum_t.tile([P, BLOCKS, P], F32, tag="t")
+            if stream == IMG:
+                wt = psum_y.tile([P, BLOCKS, P], F32, name="wt", tag="y")
+            else:
+                wt = psum_t.tile([P, BLOCKS, P], F32, name="wt", tag="t")
             for c in range(BLOCKS):
                 nc.tensor.transpose(wt[:, c, :], words[:, c * P : (c + 1) * P], ident[:])
             w_t[(stream, plane)] = wt
@@ -261,7 +252,7 @@ def tile_flux2attention_pa_t_kernel(
                 return
             pair, n = divmod(t, PAIR)
             if n == 0:
-                x_grouped[pair] = ring3.tile([P, PAIR, PASSES, P, 4], BF16, align_bytes=64, name="x_grouped")
+                x_grouped[pair] = ring4.tile([P, PAIR, PASSES, P, 4], BF16, align_bytes=64, name="x_grouped")
             words = x_raw[pair][:, n, :].bitcast(F32)
             xt = psum_t.tile([P, BLOCKS, P], F32, tag="t")
             for c in range(BLOCKS):
@@ -277,7 +268,7 @@ def tile_flux2attention_pa_t_kernel(
             )
 
         def quantise_pair(pair):
-            if not is_pair(pair):
+            if not is_tile(PAIR * pair):
                 return
             stream, m = tiles[PAIR * pair]
             if m == 0:
@@ -311,156 +302,175 @@ def tile_flux2attention_pa_t_kernel(
             y[t] = acc
 
         def make_table(t):
-            if not is_tile(t) or tiles[t][0] != IMG:
+            if not is_tile(t) or is_text(t) or is_lifted(t):
                 return
-            stream = tiles[t][0]
-            tab = table_pool.tile([P, 2, 2, 2, HALF], F32, name="tab")
-            both = trig[t // TRIG_CHUNK][:, t % TRIG_CHUNK]
-            planes = both.rearrange("p cs j -> p (cs j)").rearrange("p (ci two) -> p two ci", two=2)
+            tab = table_pool.tile([P, 2, 2, HEAD], F32, name="tab")
             nc.vector.tensor_tensor(
-                out=tab[:].rearrange("p q two cs i -> p q two (cs i)"),
-                in0=planes.unsqueeze(1).to_broadcast([P, 2, 2, HEAD]),
-                in1=gains[:, stream, :].rearrange("p (q two c) -> p q two c", q=2, two=2),
+                out=tab[:],
+                in0=trig[tiles[t]].unsqueeze(2).to_broadcast([P, 2, 2, HEAD]),
+                in1=gains[:, IMG, :].rearrange("p (cs q d) -> p cs q d", cs=2, q=2),
                 op=ALU.mult,
             )
             table[t] = tab
 
+        def transpose_trig(ts):
+            bank = psum_x.tile([P, len(ts), 2, P], BF16, name="trig_bank", tag="x")
+            for n, t in enumerate(ts):
+                for cs in range(2):
+                    nc.tensor.transpose(bank[:, n, cs, :], trig[tiles[t]][:, cs, :], ident_bf[:])
+            return bank
+
+        def keep_trig(ts, bank):
+            kept = ring3.tile([P, len(LIFT_PLACES), 2, P], BF16, name="trig_t")
+            nc.scalar.copy(out=kept[:, : len(ts)], in_=bank[:])
+            for n, t in enumerate(ts):
+                trig_t[t] = kept[:, n]
+
         def project_table(t):
-            if not is_tile(t) or tiles[t][0] != TXT:
-                return
-            m = tiles[t][1]
-            tab = psum_y.tile([P, 2, 2, 2, HALF], F32, tag="y")
+            tab = psum_x.tile([P, 2, 2, HEAD], F32, name="table_bank", tag="x")
             for cs in range(2):
                 nc.tensor.matmul(
-                    out=tab[:].rearrange("p q two cs i -> p (q two cs i)"),
-                    lhsT=trig_t[cs][:, m, :],
-                    rhs=diagonal[:, cs, :],
-                    start=(cs == 0),
-                    stop=(cs == 1),
+                    out=tab[:, cs].rearrange("p q d -> p (q d)"),
+                    lhsT=trig_t[t][:, cs, :],
+                    rhs=diagonal[tiles[t][0]][:, cs].rearrange("p q d -> p (q d)"),
+                    start=True,
+                    stop=True,
                 )
             table[t] = tab
 
+        def keep_table(t):
+            tab = ring6.tile([P, 2, 2, HEAD], F32, name="kept_table")
+            nc.scalar.copy(out=tab[:], in_=table[t][:])
+            table[t] = tab
+
         def add_bias(t):
-            if not is_tile(t) or tiles[t][0] != TXT:
+            if not is_text(t):
                 return
             biased = ring4.tile([P, OUTS], F32, name="biased")
             nc.vector.tensor_tensor(out=biased[:], in0=y[t][:], in1=bias[:], op=ALU.add)
             y[t] = biased
 
-        def by_plane(ap):
-            return ap.rearrange("p (q two h i) -> p q two h i", q=2, two=2, h=2)
-
         def sum_squares(t):
             if not is_tile(t):
                 return
             squares = ring3.tile([P, OUTS], BF16, name="squares")
-            sums = ring6.tile([P, 4], F32, name="sums")
-            for q in range(2):
-                for h in range(2):
-                    nc.scalar.activation(
-                        out=by_plane(squares[:])[:, q, :, h, :],
-                        in_=by_plane(y[t][:])[:, q, :, h, :],
-                        func=ACT.Square,
-                        accum_out=sums[:, 2 * q + h : 2 * q + h + 1],
-                    )
+            sums = ring6.tile([P, PLANES], F32, name="sums")
+            for v in range(PLANES):
+                nc.scalar.activation(
+                    out=squares[:, v * HEAD : (v + 1) * HEAD],
+                    in_=y[t][:, v * HEAD : (v + 1) * HEAD],
+                    func=ACT.Square,
+                    accum_out=sums[:, v : v + 1],
+                )
             sumsq[t] = sums
 
         def inverse_rms(t):
             if not is_tile(t):
                 return
-            r = ring6.tile([P, 4], F32, name="r")
+            r = ring6.tile([P, PLANES], F32, name="r")
             nc.scalar.activation(out=r[:], in_=sumsq[t][:], func=ACT.Abs_reciprocal_sqrt, bias=EPS, scale=1.0 / HEAD)
             rstd[t] = r
+
+        def by_pair(ap):
+            return ap.rearrange("p (i two) -> p i two", two=2)
 
         def multiply(t):
             if not is_tile(t):
                 return
-            tab = table[t]
             a = ring3.tile([P, OUTS], F32, name="a")
-            nc.vector.tensor_tensor(
-                out=a[:].rearrange("p (v h i) -> p v h i", v=PLANES, h=2),
-                in0=y[t][:].rearrange("p (v h i) -> p v h i", v=PLANES, h=2),
-                in1=tab[:, :, :, 0, :].rearrange("p q two i -> p (q two) i").unsqueeze(2).to_broadcast([P, PLANES, 2, HALF]),
-                op=ALU.mult,
-            )
             b = ring3.tile([P, OUTS], F32, name="b")
-            for two in range(2):
-                nc.vector.tensor_tensor(
-                    out=by_plane(b[:])[:, :, two],
-                    in0=by_plane(y[t][:])[:, :, 1 - two],
-                    in1=tab[:, :, two, 1, :].unsqueeze(2).to_broadcast([P, 2, 2, HALF]),
-                    op=ALU.mult,
+            for v in range(PLANES):
+                cols = slice(v * HEAD, (v + 1) * HEAD)
+                nc.vector.scalar_tensor_tensor(
+                    out=a[:, cols],
+                    in0=y[t][:, cols],
+                    scalar=rstd[t][:, v : v + 1],
+                    in1=table[t][:, 0, v // 2, :],
+                    op0=ALU.mult,
+                    op1=ALU.mult,
+                )
+                nc.vector.scalar_tensor_tensor(
+                    out=by_pair(b[:, cols]),
+                    in0=by_pair(y[t][:, cols])[:, :, ::-1],
+                    scalar=rstd[t][:, v : v + 1],
+                    in1=by_pair(table[t][:, 1, v // 2, :]),
+                    op0=ALU.mult,
+                    op1=ALU.mult,
                 )
             straight[t] = a
             crossed[t] = b
 
-        def add(t, engine):
-            if not is_tile(t):
-                return
-            rot = ring3.tile([P, OUTS], F32, name="rot")
-            engine.tensor_tensor(out=rot[:], in0=straight[t][:], in1=crossed[t][:], op=ALU.add)
-            rotated[t] = rot
-
-        def scale_and_store(t):
+        def add_and_store(t, engine):
             if not is_tile(t):
                 return
             stream, m = tiles[t]
-            result = out_pool.tile([P, 2, 2, HEAD], F32, name="result")
-            for q in range(2):
-                for h in range(2):
-                    nc.scalar.activation(
-                        out=result[:, q, h, :].rearrange("p (i two) -> p i two", two=2),
-                        in_=by_plane(rotated[t][:])[:, q, :, h, :].rearrange("p two i -> p i two"),
-                        func=ACT.Copy,
-                        scale=rstd[t][:, 2 * q + h : 2 * q + h + 1],
-                    )
-            nc.sync.dma_start(out=q_dram[stream][:, m, :], in_=result[:, 0].rearrange("p h c -> p (h c)"))
-            nc.sync.dma_start(out=k_dram[stream][:, m, :], in_=result[:, 1].rearrange("p h c -> p (h c)"))
+            result = out_pool.tile([P, OUTS], F32, name="result")
+            engine.tensor_tensor(out=result[:], in0=straight[t][:], in1=crossed[t][:], op=ALU.add)
+            nc.sync.dma_start(out=q_dram[stream][:, m, :], in_=result[:, : 2 * HEAD])
+            nc.sync.dma_start(out=k_dram[stream][:, m, :], in_=result[:, 2 * HEAD :])
 
         with tc.manual_schedule():
             order_gains(IMG)
-            spread_gains(IMG)
-            for t in range(TABLE_AHEAD):
+            keep_gains(IMG, spread(IMG))
+            for t in range(EARLY_TABLES):
                 make_table(t)
-            for t in range(-WEIGHTS_AHEAD, len(tiles) + STORE_BEHIND):
-                plane = t - (first_tile[IMG] - WEIGHTS_AHEAD)
-                if 0 <= plane < PLANES:
-                    transpose_weight_plane(IMG, plane)
-                    regroup_weight_plane(IMG, plane, nc.scalar.copy)
-                step = t - (first_tile[TXT] - WEIGHTS_AHEAD)
-                if 0 <= step < PLANES:
-                    transpose_weight_plane(TXT, step)
-                if t % RUN == RUN - 1:
-                    for n in range(RUN):
-                        transpose_tile(t + TRANSPOSE_AHEAD + n)
-                if t % RUN == 0:
-                    for n in range(RUN):
-                        project_tile(t + PROJECT_AHEAD + n)
-                if (t + 1 + PROJECT_AHEAD) % PAIR == 0:
-                    quantise_pair((t + 1 + PROJECT_AHEAD) // PAIR)
-                project_table(t + TEXT_TABLE_AHEAD)
-                if t == -PROJECT_AHEAD:
+            for t in range(IMG_WEIGHTS_AT, n_all + ADD_BEHIND):
+                planes = [(s, t - at) for s, at in ((IMG, IMG_WEIGHTS_AT), (TXT, TXT_WEIGHTS_AT)) if 0 <= t - at < PLANES]
+                for s, plane in planes:
+                    transpose_weight_plane(s, plane)
+                transpose_tile(t + TRANSPOSE_AHEAD)
+                project_tile(t + PROJECT_AHEAD)
+                group, place = divmod(t, GROUP)
+                base = GROUP * group
+                turned = []
+                lifted = None
+                if t >= 0:
+                    if place < 4:
+                        lifted = base + LIFT_PLACES[place]
+                    elif place == 4:
+                        turned = [base + n for n in TEXT_PLACES]
+                    elif place < 7:
+                        project_table(base + TEXT_PLACES[place - 5])
+                    else:
+                        turned = [base + GROUP + n for n in LIFT_PLACES]
+                turned = [u for u in turned if is_tile(u)]
+                if turned:
+                    bank = transpose_trig(turned)
+                if lifted is not None and is_lifted(lifted):
+                    project_table(lifted)
+                if t == 0:
                     order_gains(TXT)
                     order_bias()
-                if step == 0:
-                    spread_gains(TXT)
-                    bias_ps = spread_bias()
-                if step == 1:
-                    nc.vector.tensor_copy(out=bias[:], in_=bias_ps[:])
-                    gains_on_diagonal()
-                if 1 <= step < PLANES + 1:
-                    regroup_weight_plane(TXT, step - 1, nc.vector.tensor_copy if step % 2 == 0 else nc.scalar.copy)
-                for cs in range(2):
-                    if step == PLANES + cs:
-                        trig_bank = transpose_trig(cs)
-                    if step == PLANES + cs + 1:
-                        keep_trig(cs, trig_bank)
+                    text_banks = (spread(TXT), spread(2))
+
+                if (IMG, 3) in planes:
+                    regroup_weight_plane(IMG, 3, nc.vector.tensor_copy)
+                if (t + 1 + PROJECT_AHEAD) % PAIR == 0:
+                    quantise_pair((t + 1 + PROJECT_AHEAD) // PAIR)
+                if t == -3:
+                    for u in range(EARLY_TABLES, GROUP):
+                        make_table(u)
+                if t == 1:
+                    keep_gains(TXT, text_banks[0])
+                    nc.vector.tensor_copy(out=bias[:], in_=text_banks[1][:])
+                if t == 2:
+                    gains_on_diagonal(TXT)
+                if t == 3:
+                    gains_on_diagonal(IMG)
                 add_bias(t + BIAS_AHEAD)
-                if t >= 0:
+                if t + TABLE_AHEAD >= GROUP:
                     make_table(t + TABLE_AHEAD)
                 multiply(t)
-                add(t - ADD_BEHIND, nc.gpsimd if is_tile(t) else nc.vector)
-                regroup(t + TRANSPOSE_AHEAD)
-                sum_squares(t + NORM_AHEAD)
-                scale_and_store(t - STORE_BEHIND)
+
+                add_and_store(t - ADD_BEHIND, nc.gpsimd if is_tile(t) else nc.vector)
+
                 inverse_rms(t + NORM_AHEAD)
+                sum_squares(t + SQUARES_AHEAD)
+                for s, plane in planes:
+                    if (s, plane) != (IMG, 3):
+                        regroup_weight_plane(s, plane, nc.scalar.copy)
+                regroup(t + TRANSPOSE_AHEAD)
+                if turned:
+                    keep_trig(turned, bank)
+                if lifted is not None and is_lifted(lifted):
+                    keep_table(lifted)

@@ -171,8 +171,8 @@ def tile_flux2attention_pa_t_kernel(
             pairs = w.rearrange("p (ci two) -> p ci two", two=2)
             beside_sin = g[:, 1, :].rearrange("p (ci two) -> p ci two", two=2)
             nc.vector.tensor_copy(out=g[:, 0, :], in_=w)
-            nc.vector.tensor_scalar_mul(out=beside_sin[:, :, 0], in0=pairs[:, :, 1], scalar1=-1.0)
-            nc.vector.tensor_copy(out=beside_sin[:, :, 1], in_=pairs[:, :, 0])
+            nc.vector.tensor_copy(out=beside_sin[:, :, 0], in_=pairs[:, :, 0])
+            nc.vector.tensor_scalar_mul(out=beside_sin[:, :, 1], in0=pairs[:, :, 1], scalar1=-1.0)
 
         def order_bias():
             nc.vector.tensor_copy(out=ordered[0:1, 2, :], in_=vectors[:, OUTS : 2 * OUTS])
@@ -185,13 +185,20 @@ def tile_flux2attention_pa_t_kernel(
         def keep_gains(stream, bank):
             nc.vector.tensor_copy(out=gains[:, stream, :], in_=bank[:])
 
+        def by_pair(ap):
+            return ap.rearrange("p (i two) -> p i two", two=2)
+
+        def gains_times(out, stream, cos, sin):
+            for cs, values in ((0, by_pair(cos)), (1, by_pair(sin)[:, :, ::-1])):
+                nc.vector.tensor_tensor(
+                    out=out[:, cs].rearrange("p q (i two) -> p q i two", two=2),
+                    in0=values.unsqueeze(1).to_broadcast([P, 2, HEAD // 2, 2]),
+                    in1=gains[:, stream, :].rearrange("p (cs q i two) -> p cs q i two", cs=2, q=2, two=2)[:, cs],
+                    op=ALU.mult,
+                )
+
         def gains_on_diagonal(stream):
-            nc.vector.tensor_tensor(
-                out=diagonal[stream][:],
-                in0=gains[:, stream, :].rearrange("p (cs q d) -> p cs q d", cs=2, q=2),
-                in1=ident_bf[:].unsqueeze(1).unsqueeze(1).to_broadcast([P, 2, 2, HEAD]),
-                op=ALU.mult,
-            )
+            gains_times(diagonal[stream], stream, ident_bf[:], ident_bf[:])
 
         w_grouped = {}
         w_t = {}
@@ -206,8 +213,7 @@ def tile_flux2attention_pa_t_kernel(
         y = {}
         sumsq = {}
         rstd = {}
-        straight = {}
-        crossed = {}
+        products = {}
 
         def is_tile(t):
             return 0 <= t < n_all
@@ -305,12 +311,7 @@ def tile_flux2attention_pa_t_kernel(
             if not is_tile(t) or is_text(t) or is_lifted(t):
                 return
             tab = table_pool.tile([P, 2, 2, HEAD], F32, name="tab")
-            nc.vector.tensor_tensor(
-                out=tab[:],
-                in0=trig[tiles[t]].unsqueeze(2).to_broadcast([P, 2, 2, HEAD]),
-                in1=gains[:, IMG, :].rearrange("p (cs q d) -> p cs q d", cs=2, q=2),
-                op=ALU.mult,
-            )
+            gains_times(tab, IMG, trig[tiles[t]][:, 0, :], trig[tiles[t]][:, 1, :])
             table[t] = tab
 
         def transpose_trig(ts):
@@ -371,41 +372,30 @@ def tile_flux2attention_pa_t_kernel(
             nc.scalar.activation(out=r[:], in_=sumsq[t][:], func=ACT.Abs_reciprocal_sqrt, bias=EPS, scale=1.0 / HEAD)
             rstd[t] = r
 
-        def by_pair(ap):
-            return ap.rearrange("p (i two) -> p i two", two=2)
-
         def multiply(t):
             if not is_tile(t):
                 return
-            a = ring3.tile([P, OUTS], F32, name="a")
-            b = ring3.tile([P, OUTS], F32, name="b")
+            both = ring3.tile([P, 2, PLANES, HEAD], F32, name="both")
             for v in range(PLANES):
-                cols = slice(v * HEAD, (v + 1) * HEAD)
                 nc.vector.scalar_tensor_tensor(
-                    out=a[:, cols],
-                    in0=y[t][:, cols],
+                    out=both[:, :, v, :],
+                    in0=y[t][:, v * HEAD : (v + 1) * HEAD].unsqueeze(1).to_broadcast([P, 2, HEAD]),
                     scalar=rstd[t][:, v : v + 1],
-                    in1=table[t][:, 0, v // 2, :],
+                    in1=table[t][:, :, v // 2, :],
                     op0=ALU.mult,
                     op1=ALU.mult,
                 )
-                nc.vector.scalar_tensor_tensor(
-                    out=by_pair(b[:, cols]),
-                    in0=by_pair(y[t][:, cols])[:, :, ::-1],
-                    scalar=rstd[t][:, v : v + 1],
-                    in1=by_pair(table[t][:, 1, v // 2, :]),
-                    op0=ALU.mult,
-                    op1=ALU.mult,
-                )
-            straight[t] = a
-            crossed[t] = b
+            products[t] = both
 
         def add_and_store(t, engine):
             if not is_tile(t):
                 return
             stream, m = tiles[t]
             result = out_pool.tile([P, OUTS], F32, name="result")
-            engine.tensor_tensor(out=result[:], in0=straight[t][:], in1=crossed[t][:], op=ALU.add)
+            straight, crossed = (products[t][:, n].rearrange("p v d -> p (v d)") for n in range(2))
+            engine.tensor_tensor(
+                out=by_pair(result[:]), in0=by_pair(straight), in1=by_pair(crossed)[:, :, ::-1], op=ALU.add
+            )
             nc.sync.dma_start(out=q_dram[stream][:, m, :], in_=result[:, : 2 * HEAD])
             nc.sync.dma_start(out=k_dram[stream][:, m, :], in_=result[:, 2 * HEAD :])
 
@@ -438,7 +428,7 @@ def tile_flux2attention_pa_t_kernel(
                     bank = transpose_trig(turned)
                 if lifted is not None and is_lifted(lifted):
                     project_table(lifted)
-                if t == 0:
+                if t == -2:
                     order_gains(TXT)
                     order_bias()
                     text_banks = (spread(TXT), spread(2))
@@ -450,10 +440,10 @@ def tile_flux2attention_pa_t_kernel(
                 if t == -3:
                     for u in range(EARLY_TABLES, GROUP):
                         make_table(u)
-                if t == 1:
+                if t == 0:
                     keep_gains(TXT, text_banks[0])
                     nc.vector.tensor_copy(out=bias[:], in_=text_banks[1][:])
-                if t == 2:
+                if t == 1:
                     gains_on_diagonal(TXT)
                 if t == 3:
                     gains_on_diagonal(IMG)

@@ -26,16 +26,15 @@ GROUP = 8
 TEXT_PLACES = (6, 7)
 LIFT_PLACES = (2, 3, 4, 5)
 
-IMG_WEIGHTS_AT = -11
-TXT_WEIGHTS_AT = -2
+TXT_WEIGHTS_AT = 1
 TRANSPOSE_AHEAD = 7
 PROJECT_AHEAD = 3
 BIAS_AHEAD = 2
 SQUARES_AHEAD = 2
 NORM_AHEAD = 1
 ADD_BEHIND = 1
+CATCH_UP_AT = 4
 TRIG_CHUNK = 8
-EARLY_TABLES = 4
 TABLE_AHEAD = 7
 
 FLOPS = 2 * (S_TXT + S_IMG) * K * OUTS
@@ -114,15 +113,20 @@ def tile_flux2attention_pa_t_kernel(
         def load_weights(stream):
             for qk in range(2):
                 rows = w_pool.tile([P, 2, K], BF16, name="w_raw%d%d" % (stream, qk), tag="w_raw")
-                nc.sync.dma_start(out=rows[:], in_=weights[stream][qk].rearrange("(h d) k -> d h k", h=2))
+                by_head = weights[stream][qk].rearrange("(h d) k -> d h k", h=2)
                 for h in range(2):
+                    nc.sync.dma_start(out=rows[:, h, :], in_=by_head[:, h, :])
                     w_raw[(stream, 2 * qk + h)] = rows[:, h, :]
 
         def load_pairs(pairs):
             for pair in pairs:
                 stream, m = tiles[PAIR * pair]
                 rows = x_pool.tile([P, PAIR, K], BF16, name="x_raw%d" % pair, tag="x_raw")
-                nc.sync.dma_start(out=rows[:], in_=x_dram[stream][:, m : m + PAIR, :])
+                if pair == 0:
+                    for n in range(PAIR):
+                        nc.sync.dma_start(out=rows[:, n, :], in_=x_dram[stream][:, m + n, :])
+                else:
+                    nc.sync.dma_start(out=rows[:], in_=x_dram[stream][:, m : m + PAIR, :])
                 x_raw[pair] = rows
 
         def load_trig(stream, chunk):
@@ -134,17 +138,17 @@ def tile_flux2attention_pa_t_kernel(
                 trig[(stream, m + n)] = both[:, :, n, :]
 
         load_vectors((wq_norm, wk_norm), 2 * HEAD)
-        load_trig(IMG, 0)
         load_weights(IMG)
         load_pairs(range(0, 2))
+        load_trig(IMG, 0)
         load_vectors((waq_norm, wak_norm), 0)
         load_vectors((baq, bak), OUTS)
-        load_pairs(range(2, 3))
+        load_pairs(range(2, 4))
         load_weights(TXT)
-        load_pairs(range(3, 4))
         load_trig(TXT, 0)
+        load_pairs(range(4, 5))
         load_trig(IMG, 1)
-        load_pairs(range(4, 8))
+        load_pairs(range(5, 8))
         load_trig(IMG, 2)
         load_pairs(range(8, n_pairs))
 
@@ -161,7 +165,7 @@ def tile_flux2attention_pa_t_kernel(
         nc.vector.memset(ones[:], 1.0)
         ordered = const.tile([P, 3, OUTS], BF16)
         nc.vector.memset(ordered[:], 0.0)
-        gains = const.tile([P, 2, OUTS], BF16)
+        gains = const.tile([P, OUTS], BF16)
         bias = const.tile([P, OUTS], F32)
         diagonal = {s: const.tile([P, 2, 2, HEAD], BF16, name="diagonal%d" % s) for s in (IMG, TXT)}
 
@@ -182,23 +186,20 @@ def tile_flux2attention_pa_t_kernel(
             nc.tensor.matmul(out=bank[:], lhsT=ones[:], rhs=ordered[:, row, :], start=True, stop=True)
             return bank
 
-        def keep_gains(stream, bank):
-            nc.vector.tensor_copy(out=gains[:, stream, :], in_=bank[:])
-
         def by_pair(ap):
             return ap.rearrange("p (i two) -> p i two", two=2)
 
-        def gains_times(out, stream, cos, sin):
+        def gains_times(engine, out, row, cos, sin):
             for cs, values in ((0, by_pair(cos)), (1, by_pair(sin)[:, :, ::-1])):
-                nc.vector.tensor_tensor(
+                engine.tensor_tensor(
                     out=out[:, cs].rearrange("p q (i two) -> p q i two", two=2),
                     in0=values.unsqueeze(1).to_broadcast([P, 2, HEAD // 2, 2]),
-                    in1=gains[:, stream, :].rearrange("p (cs q i two) -> p cs q i two", cs=2, q=2, two=2)[:, cs],
+                    in1=row.rearrange("p (cs q i two) -> p cs q i two", cs=2, q=2, two=2)[:, cs],
                     op=ALU.mult,
                 )
 
-        def gains_on_diagonal(stream):
-            gains_times(diagonal[stream], stream, ident_bf[:], ident_bf[:])
+        def gains_on_diagonal(engine, stream, row):
+            gains_times(engine, diagonal[stream], row, ident_bf[:], ident_bf[:])
 
         w_grouped = {}
         w_t = {}
@@ -225,8 +226,11 @@ def tile_flux2attention_pa_t_kernel(
             return GROUP <= t < n_all and t % GROUP in LIFT_PLACES
 
         def transpose_weight_plane(stream, plane):
-            if plane == 0:
-                w_grouped[stream] = const.tile([P, PASSES, OUTS, 4], BF16, align_bytes=64, name="w_grouped%d" % stream)
+            qk, h = divmod(plane, 2)
+            if h == 0:
+                w_grouped[(stream, qk)] = const.tile(
+                    [P, PASSES, 2 * HEAD, 4], BF16, align_bytes=64, name="w_grouped%d%d" % (stream, qk)
+                )
             words = w_raw[(stream, plane)].bitcast(F32)
             if stream == IMG:
                 wt = psum_y.tile([P, BLOCKS, P], F32, name="wt", tag="y")
@@ -237,21 +241,23 @@ def tile_flux2attention_pa_t_kernel(
             w_t[(stream, plane)] = wt
 
         def regroup_weight_plane(stream, plane, copy):
+            qk, h = divmod(plane, 2)
             copy(
-                out=w_grouped[stream][:].bitcast(F32)[:, :, plane * P : (plane + 1) * P, :],
+                out=w_grouped[(stream, qk)][:].bitcast(F32)[:, :, h * P : (h + 1) * P, :],
                 in_=w_t[(stream, plane)][:].rearrange("p (g u) r -> p g r u", u=2),
             )
 
-        def quantise_weights(stream):
-            codes = const.tile([P, PASSES, OUTS], U32, align_bytes=64, name="w_codes%d" % stream)
-            scales = const.tile([P, PASSES, OUTS], U8, align_bytes=64, name="w_scales%d" % stream)
-            nc.vector.quantize_mx(
-                out=codes[:].rearrange("p g c -> p (g c)").bitcast(FP8X4),
-                scales=scales[:].rearrange("p g c -> p (g c)"),
-                in_=w_grouped[stream][:].rearrange("p g c j -> p (g c j)"),
-            )
-            w_codes[stream] = codes
-            w_scales[stream] = scales
+        def quantise_weights(stream, qk):
+            if qk == 0:
+                w_codes[stream] = const.tile([P, PASSES, OUTS], U32, align_bytes=64, name="w_codes%d" % stream)
+                w_scales[stream] = const.tile([P, PASSES, OUTS], U8, align_bytes=64, name="w_scales%d" % stream)
+            cols = slice(qk * 2 * HEAD, (qk + 1) * 2 * HEAD)
+            for g in range(PASSES):
+                nc.vector.quantize_mx(
+                    out=w_codes[stream][:, g, cols].bitcast(FP8X4),
+                    scales=w_scales[stream][:, g, cols],
+                    in_=w_grouped[(stream, qk)][:, g].rearrange("p c j -> p (c j)"),
+                )
 
         def transpose_tile(t):
             if not is_tile(t):
@@ -276,9 +282,6 @@ def tile_flux2attention_pa_t_kernel(
         def quantise_pair(pair):
             if not is_tile(PAIR * pair):
                 return
-            stream, m = tiles[PAIR * pair]
-            if m == 0:
-                quantise_weights(stream)
             codes = ring3.tile([P, PAIR, PASSES, P], U32, align_bytes=64, name="x_codes")
             scales = ring3.tile([P, PAIR, PASSES, P], U8, align_bytes=64, name="x_scales")
             nc.vector.quantize_mx(
@@ -307,11 +310,11 @@ def tile_flux2attention_pa_t_kernel(
                 )
             y[t] = acc
 
-        def make_table(t):
+        def make_table(t, engine):
             if not is_tile(t) or is_text(t) or is_lifted(t):
                 return
             tab = table_pool.tile([P, 2, 2, HEAD], F32, name="tab")
-            gains_times(tab, IMG, trig[tiles[t]][:, 0, :], trig[tiles[t]][:, 1, :])
+            gains_times(engine, tab, gains[:], trig[tiles[t]][:, 0, :], trig[tiles[t]][:, 1, :])
             table[t] = tab
 
         def transpose_trig(ts):
@@ -387,28 +390,44 @@ def tile_flux2attention_pa_t_kernel(
                 )
             products[t] = both
 
-        def add_and_store(t, engine):
+        def add_and_store(t, engines):
             if not is_tile(t):
                 return
             stream, m = tiles[t]
             result = out_pool.tile([P, OUTS], F32, name="result")
             straight, crossed = (products[t][:, n].rearrange("p v d -> p (v d)") for n in range(2))
-            engine.tensor_tensor(
-                out=by_pair(result[:]), in0=by_pair(straight), in1=by_pair(crossed)[:, :, ::-1], op=ALU.add
-            )
-            nc.sync.dma_start(out=q_dram[stream][:, m, :], in_=result[:, : 2 * HEAD])
-            nc.sync.dma_start(out=k_dram[stream][:, m, :], in_=result[:, 2 * HEAD :])
+            halves = [slice(0, 2 * HEAD), slice(2 * HEAD, OUTS)]
+            for eng, cols in zip(engines, halves if len(engines) == 2 else [slice(0, OUTS)]):
+                eng.tensor_tensor(
+                    out=by_pair(result[:, cols]),
+                    in0=by_pair(straight[:, cols]),
+                    in1=by_pair(crossed[:, cols])[:, :, ::-1],
+                    op=ALU.add,
+                )
+            for rows, cols in zip((q_dram, k_dram), halves):
+                nc.sync.dma_start(out=rows[stream][:, m, :], in_=result[:, cols])
 
         with tc.manual_schedule():
             order_gains(IMG)
-            keep_gains(IMG, spread(IMG))
-            for t in range(EARLY_TABLES):
-                make_table(t)
-            for t in range(IMG_WEIGHTS_AT, n_all + ADD_BEHIND):
-                planes = [(s, t - at) for s, at in ((IMG, IMG_WEIGHTS_AT), (TXT, TXT_WEIGHTS_AT)) if 0 <= t - at < PLANES]
-                for s, plane in planes:
-                    transpose_weight_plane(s, plane)
-                transpose_tile(t + TRANSPOSE_AHEAD)
+            nc.vector.tensor_copy(out=gains[:], in_=spread(IMG)[:])
+            gains_on_diagonal(nc.gpsimd, IMG, gains[:])
+            for plane in range(PLANES):
+                transpose_weight_plane(IMG, plane)
+                if plane % 2 == 0:
+                    regroup_weight_plane(IMG, plane, nc.scalar.copy)
+                else:
+                    regroup_weight_plane(IMG, plane, nc.vector.tensor_copy)
+                    quantise_weights(IMG, plane // 2)
+            for t in range(-TRANSPOSE_AHEAD, n_all + ADD_BEHIND):
+                if t < -PROJECT_AHEAD:
+                    fresh = [t + TRANSPOSE_AHEAD]
+                elif t <= CATCH_UP_AT:
+                    fresh = [t + TRANSPOSE_AHEAD - 1] if t > -PROJECT_AHEAD else []
+                    fresh += [t + TRANSPOSE_AHEAD] if t == CATCH_UP_AT else []
+                else:
+                    fresh = [t + TRANSPOSE_AHEAD]
+                for u in fresh:
+                    transpose_tile(u)
                 project_tile(t + PROJECT_AHEAD)
                 group, place = divmod(t, GROUP)
                 base = GROUP * group
@@ -428,39 +447,45 @@ def tile_flux2attention_pa_t_kernel(
                     bank = transpose_trig(turned)
                 if lifted is not None and is_lifted(lifted):
                     project_table(lifted)
-                if t == -2:
+                if t == -1:
                     order_gains(TXT)
                     order_bias()
                     text_banks = (spread(TXT), spread(2))
 
-                if (IMG, 3) in planes:
-                    regroup_weight_plane(IMG, 3, nc.vector.tensor_copy)
-                if (t + 1 + PROJECT_AHEAD) % PAIR == 0:
-                    quantise_pair((t + 1 + PROJECT_AHEAD) // PAIR)
-                if t == -3:
-                    for u in range(EARLY_TABLES, GROUP):
-                        make_table(u)
-                if t == 0:
-                    keep_gains(TXT, text_banks[0])
-                    nc.vector.tensor_copy(out=bias[:], in_=text_banks[1][:])
-                if t == 1:
-                    gains_on_diagonal(TXT)
+                pair, odd = divmod(t + 1 + PROJECT_AHEAD, PAIR)
+                if odd == 0 and not 0 <= t <= TXT_WEIGHTS_AT + 1:
+                    quantise_pair(pair)
+                if t == -PROJECT_AHEAD - 1:
+                    for u in range(4):
+                        make_table(u, nc.vector)
+                    for u in range(4, GROUP + 2):
+                        make_table(u, nc.gpsimd)
                 if t == 3:
-                    gains_on_diagonal(IMG)
+                    gains_on_diagonal(nc.vector, TXT, text_banks[0][:])
                 add_bias(t + BIAS_AHEAD)
-                if t + TABLE_AHEAD >= GROUP:
-                    make_table(t + TABLE_AHEAD)
+                if t + TABLE_AHEAD >= GROUP + 2:
+                    make_table(t + TABLE_AHEAD, nc.vector)
                 multiply(t)
 
-                add_and_store(t - ADD_BEHIND, nc.gpsimd if is_tile(t) else nc.vector)
+                add_and_store(t - ADD_BEHIND, (nc.gpsimd,) if is_tile(t) else (nc.gpsimd, nc.vector))
 
                 inverse_rms(t + NORM_AHEAD)
                 sum_squares(t + SQUARES_AHEAD)
-                for s, plane in planes:
-                    if (s, plane) != (IMG, 3):
-                        regroup_weight_plane(s, plane, nc.scalar.copy)
-                regroup(t + TRANSPOSE_AHEAD)
+                for u in fresh:
+                    regroup(u)
                 if turned:
                     keep_trig(turned, bank)
                 if lifted is not None and is_lifted(lifted):
                     keep_table(lifted)
+                if t == 2:
+                    nc.scalar.copy(out=bias[:], in_=text_banks[1][:])
+
+                if TXT_WEIGHTS_AT <= t + 1 <= TXT_WEIGHTS_AT + 1:
+                    for plane in range(2 * (t + 1 - TXT_WEIGHTS_AT), 2 * (t + 2 - TXT_WEIGHTS_AT)):
+                        transpose_weight_plane(TXT, plane)
+                        regroup_weight_plane(TXT, plane, nc.scalar.copy)
+                if t == TXT_WEIGHTS_AT + 1:
+                    for qk in range(2):
+                        quantise_weights(TXT, qk)
+                if odd == 0 and 0 <= t <= TXT_WEIGHTS_AT + 1:
+                    quantise_pair(pair)

@@ -35,7 +35,6 @@ NORM_AHEAD = 1
 ADD_BEHIND = 1
 CATCH_UP_AT = 4
 TRIG_CHUNK = 8
-TABLE_AHEAD = 7
 
 FLOPS = 2 * (S_TXT + S_IMG) * K * OUTS
 
@@ -189,8 +188,9 @@ def tile_flux2attention_pa_t_kernel(
         def by_pair(ap):
             return ap.rearrange("p (i two) -> p i two", two=2)
 
-        def gains_times(engine, out, row, cos, sin):
-            for cs, values in ((0, by_pair(cos)), (1, by_pair(sin)[:, :, ::-1])):
+        def gains_times(engine, out, row, cos, sin, parts=(0, 1)):
+            for cs in parts:
+                values = by_pair(cos) if cs == 0 else by_pair(sin)[:, :, ::-1]
                 engine.tensor_tensor(
                     out=out[:, cs].rearrange("p q (i two) -> p q i two", two=2),
                     in0=values.unsqueeze(1).to_broadcast([P, 2, HEAD // 2, 2]),
@@ -310,12 +310,10 @@ def tile_flux2attention_pa_t_kernel(
                 )
             y[t] = acc
 
-        def make_table(t, engine):
-            if not is_tile(t) or is_text(t) or is_lifted(t):
-                return
-            tab = table_pool.tile([P, 2, 2, HEAD], F32, name="tab")
-            gains_times(engine, tab, gains[:], trig[tiles[t]][:, 0, :], trig[tiles[t]][:, 1, :])
-            table[t] = tab
+        def make_table(t, engine, row, parts=(0, 1)):
+            if 0 in parts:
+                table[t] = table_pool.tile([P, 2, 2, HEAD], F32, name="tab")
+            gains_times(engine, table[t], row, trig[tiles[t]][:, 0, :], trig[tiles[t]][:, 1, :], parts)
 
         def transpose_trig(ts):
             bank = psum_x.tile([P, len(ts), 2, P], BF16, name="trig_bank", tag="x")
@@ -408,8 +406,10 @@ def tile_flux2attention_pa_t_kernel(
                 nc.sync.dma_start(out=rows[stream][:, m, :], in_=result[:, cols])
 
         with tc.manual_schedule():
+            halves = [(u, cs) for u in range(GROUP, n_all) if not is_text(u) and not is_lifted(u) for cs in range(2)]
             order_gains(IMG)
-            nc.vector.tensor_copy(out=gains[:], in_=spread(IMG)[:])
+            gains_bank = spread(IMG)
+            nc.vector.tensor_copy(out=gains[:], in_=gains_bank[:])
             gains_on_diagonal(nc.gpsimd, IMG, gains[:])
             for plane in range(PLANES):
                 transpose_weight_plane(IMG, plane)
@@ -456,18 +456,21 @@ def tile_flux2attention_pa_t_kernel(
                 if odd == 0 and not 0 <= t <= TXT_WEIGHTS_AT + 1:
                     quantise_pair(pair)
                 if t == -PROJECT_AHEAD - 1:
-                    for u in range(4):
-                        make_table(u, nc.vector)
-                    for u in range(4, GROUP + 2):
-                        make_table(u, nc.gpsimd)
+                    for u in range(TEXT_PLACES[0]):
+                        if u < 4:
+                            make_table(u, nc.vector, gains_bank[:])
+                        else:
+                            make_table(u, nc.gpsimd, gains[:])
                 if t == 3:
                     gains_on_diagonal(nc.vector, TXT, text_banks[0][:])
                 add_bias(t + BIAS_AHEAD)
-                if t + TABLE_AHEAD >= GROUP + 2:
-                    make_table(t + TABLE_AHEAD, nc.vector)
                 multiply(t)
 
                 add_and_store(t - ADD_BEHIND, (nc.gpsimd,) if is_tile(t) else (nc.gpsimd, nc.vector))
+
+                if t > 0 and t % PAIR == 1 and t // PAIR < len(halves):
+                    u, cs = halves[t // PAIR]
+                    make_table(u, nc.gpsimd, gains[:], (cs,))
 
                 inverse_rms(t + NORM_AHEAD)
                 sum_squares(t + SQUARES_AHEAD)

@@ -25,6 +25,7 @@ PAIR = 2
 GROUP = 8
 TEXT_PLACES = (6, 7)
 LIFT_PLACES = (2, 3, 4, 5)
+FIRST_LIFTS = (8, 9)
 
 TXT_WEIGHTS_AT = 1
 TRANSPOSE_AHEAD = 7
@@ -91,8 +92,8 @@ def tile_flux2attention_pa_t_kernel(
         ring3 = ctx.enter_context(tc.tile_pool(name="ring3", bufs=3))
         ring4 = ctx.enter_context(tc.tile_pool(name="ring4", bufs=4))
         ring6 = ctx.enter_context(tc.tile_pool(name="ring6", bufs=6))
-        out_pool = ctx.enter_context(tc.tile_pool(name="out_pool", bufs=8))
-        table_pool = ctx.enter_context(tc.tile_pool(name="table_pool", bufs=9))
+        out_pool = ctx.enter_context(tc.tile_pool(name="out_pool", bufs=10))
+        table_pool = ctx.enter_context(tc.tile_pool(name="table_pool", bufs=6))
         psum_t = ctx.enter_context(tc.psum_pool(name="psum_t", bufs=2))
         psum_y = ctx.enter_context(tc.psum_pool(name="psum_y", bufs=4))
         psum_x = ctx.enter_context(tc.psum_pool(name="psum_x", bufs=2))
@@ -223,7 +224,7 @@ def tile_flux2attention_pa_t_kernel(
             return is_tile(t) and tiles[t][0] == TXT
 
         def is_lifted(t):
-            return GROUP <= t < n_all and t % GROUP in LIFT_PLACES
+            return t in FIRST_LIFTS or (GROUP <= t < n_all and t % GROUP in LIFT_PLACES)
 
         def transpose_weight_plane(stream, plane):
             qk, h = divmod(plane, 2)
@@ -434,7 +435,12 @@ def tile_flux2attention_pa_t_kernel(
                 turned = []
                 lifted = None
                 if t >= 0:
-                    if place < 4:
+                    if group == 0 and place < 4:
+                        if place == 1:
+                            turned = list(FIRST_LIFTS)
+                        elif place > 1:
+                            lifted = FIRST_LIFTS[place - 2]
+                    elif place < 4:
                         lifted = base + LIFT_PLACES[place]
                     elif place == 4:
                         turned = [base + n for n in TEXT_PLACES]
@@ -461,16 +467,15 @@ def tile_flux2attention_pa_t_kernel(
                             make_table(u, nc.vector, gains_bank[:])
                         else:
                             make_table(u, nc.gpsimd, gains[:])
-                if t == 3:
-                    gains_on_diagonal(nc.vector, TXT, text_banks[0][:])
+                if t > 1 and odd == 1 and t // PAIR <= len(halves):
+                    u, cs = halves[t // PAIR - 1]
+                    make_table(u, nc.vector, gains[:], (cs,))
                 add_bias(t + BIAS_AHEAD)
                 multiply(t)
+                if t == 0:
+                    gains_on_diagonal(nc.vector, TXT, text_banks[0][:])
 
                 add_and_store(t - ADD_BEHIND, (nc.gpsimd,) if is_tile(t) else (nc.gpsimd, nc.vector))
-
-                if t > 0 and t % PAIR == 1 and t // PAIR < len(halves):
-                    u, cs = halves[t // PAIR]
-                    make_table(u, nc.gpsimd, gains[:], (cs,))
 
                 inverse_rms(t + NORM_AHEAD)
                 sum_squares(t + SQUARES_AHEAD)
@@ -480,7 +485,7 @@ def tile_flux2attention_pa_t_kernel(
                     keep_trig(turned, bank)
                 if lifted is not None and is_lifted(lifted):
                     keep_table(lifted)
-                if t == 2:
+                if t == -1:
                     nc.scalar.copy(out=bias[:], in_=text_banks[1][:])
 
                 if TXT_WEIGHTS_AT <= t + 1 <= TXT_WEIGHTS_AT + 1:

@@ -22,15 +22,16 @@ S_TXT = 1024
 S_IMG = 3072
 EPS = 1e-5
 PAIR = 2
-GROUP = 8
-TEXT_PLACES = (6, 7)
-LIFT_PLACES = (2, 3, 4, 5)
-FIRST_LIFTS = (8, 9)
+BEAT = 4
+FIRST_TEXT = 8
+MORE_TEXT = (22, 30)
+EARLY_TABLES = 7
+FIRST_LIFT = 7
 
-TXT_WEIGHTS_AT = 1
+TXT_WEIGHTS_AT = 3
 TRANSPOSE_AHEAD = 7
 PROJECT_AHEAD = 3
-BIAS_AHEAD = 2
+BIAS_AHEAD = 3
 SQUARES_AHEAD = 2
 NORM_AHEAD = 1
 ADD_BEHIND = 1
@@ -79,9 +80,10 @@ def tile_flux2attention_pa_t_kernel(
     k_dram = (by_partition(k_rows, TXT), by_partition(k_rows, IMG))
 
     n_all = n_tiles[TXT] + n_tiles[IMG]
+    text_tiles = list(range(FIRST_TEXT, n_all, BEAT)) + list(MORE_TEXT)
     tiles = []
     for t in range(n_all):
-        stream = TXT if t % GROUP in TEXT_PLACES else IMG
+        stream = TXT if t in text_tiles else IMG
         tiles.append((stream, len([s for s, m in tiles if s == stream])))
     n_pairs = n_all // PAIR
 
@@ -93,7 +95,7 @@ def tile_flux2attention_pa_t_kernel(
         ring4 = ctx.enter_context(tc.tile_pool(name="ring4", bufs=4))
         ring6 = ctx.enter_context(tc.tile_pool(name="ring6", bufs=6))
         out_pool = ctx.enter_context(tc.tile_pool(name="out_pool", bufs=10))
-        table_pool = ctx.enter_context(tc.tile_pool(name="table_pool", bufs=6))
+        table_pool = ctx.enter_context(tc.tile_pool(name="table_pool", bufs=7))
         psum_t = ctx.enter_context(tc.psum_pool(name="psum_t", bufs=2))
         psum_y = ctx.enter_context(tc.psum_pool(name="psum_y", bufs=4))
         psum_x = ctx.enter_context(tc.psum_pool(name="psum_x", bufs=2))
@@ -118,16 +120,19 @@ def tile_flux2attention_pa_t_kernel(
                     nc.sync.dma_start(out=rows[:, h, :], in_=by_head[:, h, :])
                     w_raw[(stream, 2 * qk + h)] = rows[:, h, :]
 
-        def load_pairs(pairs):
-            for pair in pairs:
-                stream, m = tiles[PAIR * pair]
-                rows = x_pool.tile([P, PAIR, K], BF16, name="x_raw%d" % pair, tag="x_raw")
-                if pair == 0:
+        def load_tiles(ts):
+            for t in ts:
+                stream, m = tiles[t]
+                if tiles[t] in x_raw:
+                    continue
+                rows = x_pool.tile([P, PAIR, K], BF16, name="x_raw%d" % t, tag="x_raw")
+                if t == 0:
                     for n in range(PAIR):
                         nc.sync.dma_start(out=rows[:, n, :], in_=x_dram[stream][:, m + n, :])
                 else:
                     nc.sync.dma_start(out=rows[:], in_=x_dram[stream][:, m : m + PAIR, :])
-                x_raw[pair] = rows
+                for n in range(PAIR):
+                    x_raw[(stream, m + n)] = rows[:, n, :]
 
         def load_trig(stream, chunk):
             m = chunk * TRIG_CHUNK
@@ -139,18 +144,19 @@ def tile_flux2attention_pa_t_kernel(
 
         load_vectors((wq_norm, wk_norm), 2 * HEAD)
         load_weights(IMG)
-        load_pairs(range(0, 2))
+        load_tiles(range(0, 4))
         load_trig(IMG, 0)
+        load_tiles(range(4, 6))
         load_vectors((waq_norm, wak_norm), 0)
         load_vectors((baq, bak), OUTS)
-        load_pairs(range(2, 4))
+        load_tiles(range(6, 8))
         load_weights(TXT)
+        load_tiles(range(8, 9))
         load_trig(TXT, 0)
-        load_pairs(range(4, 5))
         load_trig(IMG, 1)
-        load_pairs(range(5, 8))
+        load_tiles(range(9, 17))
         load_trig(IMG, 2)
-        load_pairs(range(8, n_pairs))
+        load_tiles(range(17, n_all))
 
         one = const.tile([P, 1], F32)
         nc.vector.memset(one[:], 1.0)
@@ -224,7 +230,7 @@ def tile_flux2attention_pa_t_kernel(
             return is_tile(t) and tiles[t][0] == TXT
 
         def is_lifted(t):
-            return t in FIRST_LIFTS or (GROUP <= t < n_all and t % GROUP in LIFT_PLACES)
+            return FIRST_LIFT <= t < n_all and t % 2 == 1
 
         def transpose_weight_plane(stream, plane):
             qk, h = divmod(plane, 2)
@@ -236,7 +242,7 @@ def tile_flux2attention_pa_t_kernel(
             if stream == IMG:
                 wt = psum_y.tile([P, BLOCKS, P], F32, name="wt", tag="y")
             else:
-                wt = psum_t.tile([P, BLOCKS, P], F32, name="wt", tag="t")
+                wt = psum_x.tile([P, BLOCKS, P], F32, name="wt", tag="x")
             for c in range(BLOCKS):
                 nc.tensor.transpose(wt[:, c, :], words[:, c * P : (c + 1) * P], ident[:])
             w_t[(stream, plane)] = wt
@@ -266,7 +272,7 @@ def tile_flux2attention_pa_t_kernel(
             pair, n = divmod(t, PAIR)
             if n == 0:
                 x_grouped[pair] = ring4.tile([P, PAIR, PASSES, P, 4], BF16, align_bytes=64, name="x_grouped")
-            words = x_raw[pair][:, n, :].bitcast(F32)
+            words = x_raw[tiles[t]].bitcast(F32)
             xt = psum_t.tile([P, BLOCKS, P], F32, tag="t")
             for c in range(BLOCKS):
                 nc.tensor.transpose(xt[:, c, :], words[:, c * P : (c + 1) * P], ident[:])
@@ -324,7 +330,7 @@ def tile_flux2attention_pa_t_kernel(
             return bank
 
         def keep_trig(ts, bank):
-            kept = ring3.tile([P, len(LIFT_PLACES), 2, P], BF16, name="trig_t")
+            kept = ring3.tile([P, BEAT, 2, P], BF16, name="trig_t")
             nc.scalar.copy(out=kept[:, : len(ts)], in_=bank[:])
             for n, t in enumerate(ts):
                 trig_t[t] = kept[:, n]
@@ -407,7 +413,7 @@ def tile_flux2attention_pa_t_kernel(
                 nc.sync.dma_start(out=rows[stream][:, m, :], in_=result[:, cols])
 
         with tc.manual_schedule():
-            halves = [(u, cs) for u in range(GROUP, n_all) if not is_text(u) and not is_lifted(u) for cs in range(2)]
+            halves = [(u, cs) for u in range(EARLY_TABLES, n_all) if not is_text(u) and not is_lifted(u) for cs in range(2)]
             order_gains(IMG)
             gains_bank = spread(IMG)
             nc.vector.tensor_copy(out=gains[:], in_=gains_bank[:])
@@ -430,29 +436,17 @@ def tile_flux2attention_pa_t_kernel(
                 for u in fresh:
                     transpose_tile(u)
                 project_tile(t + PROJECT_AHEAD)
-                group, place = divmod(t, GROUP)
-                base = GROUP * group
                 turned = []
-                lifted = None
-                if t >= 0:
-                    if group == 0 and place < 4:
-                        if place == 1:
-                            turned = list(FIRST_LIFTS)
-                        elif place > 1:
-                            lifted = FIRST_LIFTS[place - 2]
-                    elif place < 4:
-                        lifted = base + LIFT_PLACES[place]
-                    elif place == 4:
-                        turned = [base + n for n in TEXT_PLACES]
-                    elif place < 7:
-                        project_table(base + TEXT_PLACES[place - 5])
-                    else:
-                        turned = [base + GROUP + n for n in LIFT_PLACES]
-                turned = [u for u in turned if is_tile(u)]
+                if t % BEAT == FIRST_TEXT % BEAT:
+                    turned = [u for u in range(t + 2, t + 2 + BEAT) if is_text(u) or is_lifted(u)]
                 if turned:
                     bank = transpose_trig(turned)
-                if lifted is not None and is_lifted(lifted):
+                lifted = {1: t + 2, 2: t + 3}.get((t - FIRST_TEXT) % BEAT)
+                lifted = lifted if lifted is not None and is_lifted(lifted) and t > 0 else None
+                if lifted is not None:
                     project_table(lifted)
+                if is_text(t + 1):
+                    project_table(t + 1)
                 if t == -1:
                     order_gains(TXT)
                     order_bias()
@@ -462,7 +456,7 @@ def tile_flux2attention_pa_t_kernel(
                 if odd == 0 and not 0 <= t <= TXT_WEIGHTS_AT + 1:
                     quantise_pair(pair)
                 if t == -PROJECT_AHEAD - 1:
-                    for u in range(TEXT_PLACES[0]):
+                    for u in range(EARLY_TABLES):
                         if u < 4:
                             make_table(u, nc.vector, gains_bank[:])
                         else:
@@ -470,8 +464,8 @@ def tile_flux2attention_pa_t_kernel(
                 if t > 1 and odd == 1 and t // PAIR <= len(halves):
                     u, cs = halves[t // PAIR - 1]
                     make_table(u, nc.vector, gains[:], (cs,))
-                add_bias(t + BIAS_AHEAD)
                 multiply(t)
+                add_bias(t + BIAS_AHEAD)
                 if t == 0:
                     gains_on_diagonal(nc.vector, TXT, text_banks[0][:])
 
@@ -483,7 +477,7 @@ def tile_flux2attention_pa_t_kernel(
                     regroup(u)
                 if turned:
                     keep_trig(turned, bank)
-                if lifted is not None and is_lifted(lifted):
+                if lifted is not None:
                     keep_table(lifted)
                 if t == -1:
                     nc.scalar.copy(out=bias[:], in_=text_banks[1][:])

@@ -31,7 +31,7 @@ FIRST_LIFT = 7
 TXT_WEIGHTS_AT = 3
 TRANSPOSE_AHEAD = 7
 PROJECT_AHEAD = 3
-BIAS_AHEAD = 3
+BIAS_AHEAD = 2
 SQUARES_AHEAD = 2
 NORM_AHEAD = 1
 ADD_BEHIND = 1
@@ -464,8 +464,8 @@ def tile_flux2attention_pa_t_kernel(
                 if t > 1 and odd == 1 and t // PAIR <= len(halves):
                     u, cs = halves[t // PAIR - 1]
                     make_table(u, nc.vector, gains[:], (cs,))
-                multiply(t)
                 add_bias(t + BIAS_AHEAD)
+                multiply(t)
                 if t == 0:
                     gains_on_diagonal(nc.vector, TXT, text_banks[0][:])
 

@@ -23,10 +23,11 @@ S_IMG = 3072
 EPS = 1e-5
 PAIR = 2
 BEAT = 4
-FIRST_TEXT = 8
-MORE_TEXT = (22, 30)
-EARLY_TABLES = 7
-FIRST_LIFT = 7
+FIRST_TEXT = 9
+MORE_TEXT = (23, 31)
+EARLY_TABLES = 8
+LATE_TABLES = (19, 27)
+TABLE_SLOTS = (8, 6)
 
 TXT_WEIGHTS_AT = 3
 TRANSPOSE_AHEAD = 7
@@ -95,7 +96,7 @@ def tile_flux2attention_pa_t_kernel(
         ring4 = ctx.enter_context(tc.tile_pool(name="ring4", bufs=4))
         ring6 = ctx.enter_context(tc.tile_pool(name="ring6", bufs=6))
         out_pool = ctx.enter_context(tc.tile_pool(name="out_pool", bufs=10))
-        table_pool = ctx.enter_context(tc.tile_pool(name="table_pool", bufs=7))
+        table_pool = ctx.enter_context(tc.tile_pool(name="table_pool", bufs=EARLY_TABLES))
         psum_t = ctx.enter_context(tc.psum_pool(name="psum_t", bufs=2))
         psum_y = ctx.enter_context(tc.psum_pool(name="psum_y", bufs=4))
         psum_x = ctx.enter_context(tc.psum_pool(name="psum_x", bufs=2))
@@ -144,17 +145,17 @@ def tile_flux2attention_pa_t_kernel(
 
         load_vectors((wq_norm, wk_norm), 2 * HEAD)
         load_weights(IMG)
+        load_vectors((waq_norm, wak_norm), 0)
+        load_vectors((baq, bak), OUTS)
         load_tiles(range(0, 4))
         load_trig(IMG, 0)
         load_tiles(range(4, 6))
-        load_vectors((waq_norm, wak_norm), 0)
-        load_vectors((baq, bak), OUTS)
-        load_tiles(range(6, 8))
+        load_tiles(range(6, 9))
         load_weights(TXT)
-        load_tiles(range(8, 9))
+        load_tiles(range(9, 10))
         load_trig(TXT, 0)
         load_trig(IMG, 1)
-        load_tiles(range(9, 17))
+        load_tiles(range(10, 17))
         load_trig(IMG, 2)
         load_tiles(range(17, n_all))
 
@@ -230,14 +231,18 @@ def tile_flux2attention_pa_t_kernel(
             return is_tile(t) and tiles[t][0] == TXT
 
         def is_lifted(t):
-            return FIRST_LIFT <= t < n_all and t % 2 == 1
+            return EARLY_TABLES <= t < n_all and not is_text(t) and t not in LATE_TABLES
 
         def transpose_weight_plane(stream, plane):
             qk, h = divmod(plane, 2)
-            if h == 0:
-                w_grouped[(stream, qk)] = const.tile(
-                    [P, PASSES, 2 * HEAD, 4], BF16, align_bytes=64, name="w_grouped%d%d" % (stream, qk)
-                )
+            if stream == IMG and h == 0:
+                half = const.tile([P, PASSES, 2 * HEAD, 4], BF16, align_bytes=64, name="w_grouped_img%d" % qk)
+                w_grouped[(stream, qk)] = half[:]
+            if stream == TXT and plane == 0:
+                whole = const.tile([P, PASSES, OUTS, 4], BF16, align_bytes=64, name="w_grouped_txt")
+                w_grouped[stream] = whole[:]
+                for n in range(2):
+                    w_grouped[(stream, n)] = whole[:, :, n * 2 * HEAD : (n + 1) * 2 * HEAD, :]
             words = w_raw[(stream, plane)].bitcast(F32)
             if stream == IMG:
                 wt = psum_y.tile([P, BLOCKS, P], F32, name="wt", tag="y")
@@ -250,21 +255,29 @@ def tile_flux2attention_pa_t_kernel(
         def regroup_weight_plane(stream, plane, copy):
             qk, h = divmod(plane, 2)
             copy(
-                out=w_grouped[(stream, qk)][:].bitcast(F32)[:, :, h * P : (h + 1) * P, :],
+                out=w_grouped[(stream, qk)].bitcast(F32)[:, :, h * P : (h + 1) * P, :],
                 in_=w_t[(stream, plane)][:].rearrange("p (g u) r -> p g r u", u=2),
             )
 
-        def quantise_weights(stream, qk):
-            if qk == 0:
-                w_codes[stream] = const.tile([P, PASSES, OUTS], U32, align_bytes=64, name="w_codes%d" % stream)
-                w_scales[stream] = const.tile([P, PASSES, OUTS], U8, align_bytes=64, name="w_scales%d" % stream)
+        for stream in (TXT, IMG):
+            w_codes[stream] = const.tile([P, PASSES, OUTS], U32, align_bytes=64, name="w_codes%d" % stream)
+            w_scales[stream] = const.tile([P, PASSES, OUTS], U8, align_bytes=64, name="w_scales%d" % stream)
+
+        def quantise_image_weights(qk):
             cols = slice(qk * 2 * HEAD, (qk + 1) * 2 * HEAD)
             for g in range(PASSES):
                 nc.vector.quantize_mx(
-                    out=w_codes[stream][:, g, cols].bitcast(FP8X4),
-                    scales=w_scales[stream][:, g, cols],
-                    in_=w_grouped[(stream, qk)][:, g].rearrange("p c j -> p (c j)"),
+                    out=w_codes[IMG][:, g, cols].bitcast(FP8X4),
+                    scales=w_scales[IMG][:, g, cols],
+                    in_=w_grouped[(IMG, qk)][:, g].rearrange("p c j -> p (c j)"),
                 )
+
+        def quantise_text_weights():
+            nc.vector.quantize_mx(
+                out=w_codes[TXT][:].rearrange("p g c -> p (g c)").bitcast(FP8X4),
+                scales=w_scales[TXT][:].rearrange("p g c -> p (g c)"),
+                in_=w_grouped[TXT].rearrange("p g c j -> p (g c j)"),
+            )
 
         def transpose_tile(t):
             if not is_tile(t):
@@ -395,15 +408,16 @@ def tile_flux2attention_pa_t_kernel(
                 )
             products[t] = both
 
-        def add_and_store(t, engines):
+        def add_and_store(t):
             if not is_tile(t):
                 return
             stream, m = tiles[t]
             result = out_pool.tile([P, OUTS], F32, name="result")
             straight, crossed = (products[t][:, n].rearrange("p v d -> p (v d)") for n in range(2))
+            last = t == n_all - 1
             halves = [slice(0, 2 * HEAD), slice(2 * HEAD, OUTS)]
-            for eng, cols in zip(engines, halves if len(engines) == 2 else [slice(0, OUTS)]):
-                eng.tensor_tensor(
+            for cols in halves if last else [slice(0, OUTS)]:
+                (nc.vector if last else nc.gpsimd).tensor_tensor(
                     out=by_pair(result[:, cols]),
                     in0=by_pair(straight[:, cols]),
                     in1=by_pair(crossed[:, cols])[:, :, ::-1],
@@ -413,18 +427,18 @@ def tile_flux2attention_pa_t_kernel(
                 nc.sync.dma_start(out=rows[stream][:, m, :], in_=result[:, cols])
 
         with tc.manual_schedule():
-            halves = [(u, cs) for u in range(EARLY_TABLES, n_all) if not is_text(u) and not is_lifted(u) for cs in range(2)]
             order_gains(IMG)
             gains_bank = spread(IMG)
             nc.vector.tensor_copy(out=gains[:], in_=gains_bank[:])
-            gains_on_diagonal(nc.gpsimd, IMG, gains[:])
             for plane in range(PLANES):
                 transpose_weight_plane(IMG, plane)
                 if plane % 2 == 0:
                     regroup_weight_plane(IMG, plane, nc.scalar.copy)
                 else:
                     regroup_weight_plane(IMG, plane, nc.vector.tensor_copy)
-                    quantise_weights(IMG, plane // 2)
+                    quantise_image_weights(plane // 2)
+            order_gains(TXT)
+            order_bias()
             for t in range(-TRANSPOSE_AHEAD, n_all + ADD_BEHIND):
                 if t < -PROJECT_AHEAD:
                     fresh = [t + TRANSPOSE_AHEAD]
@@ -438,56 +452,55 @@ def tile_flux2attention_pa_t_kernel(
                 project_tile(t + PROJECT_AHEAD)
                 turned = []
                 if t % BEAT == FIRST_TEXT % BEAT:
-                    turned = [u for u in range(t + 2, t + 2 + BEAT) if is_text(u) or is_lifted(u)]
+                    turned = [u for u in range(t + 3, t + 3 + BEAT) if is_text(u) or is_lifted(u)]
                 if turned:
                     bank = transpose_trig(turned)
-                lifted = {1: t + 2, 2: t + 3}.get((t - FIRST_TEXT) % BEAT)
-                lifted = lifted if lifted is not None and is_lifted(lifted) and t > 0 else None
-                if lifted is not None:
-                    project_table(lifted)
+                lifted = {1: [t + 2], 2: [t + 3, t + 4]}.get((t - FIRST_TEXT) % BEAT, [])
+                lifted = [u for u in lifted if is_lifted(u)]
+                for u in lifted:
+                    project_table(u)
                 if is_text(t + 1):
                     project_table(t + 1)
                 if t == -1:
-                    order_gains(TXT)
-                    order_bias()
                     text_banks = (spread(TXT), spread(2))
 
                 pair, odd = divmod(t + 1 + PROJECT_AHEAD, PAIR)
-                if odd == 0 and not 0 <= t <= TXT_WEIGHTS_AT + 1:
+                if odd == 0 and not 0 <= t < CATCH_UP_AT:
                     quantise_pair(pair)
                 if t == -PROJECT_AHEAD - 1:
                     for u in range(EARLY_TABLES):
-                        if u < 4:
+                        if u < EARLY_TABLES // 2:
                             make_table(u, nc.vector, gains_bank[:])
                         else:
                             make_table(u, nc.gpsimd, gains[:])
-                if t > 1 and odd == 1 and t // PAIR <= len(halves):
-                    u, cs = halves[t // PAIR - 1]
-                    make_table(u, nc.vector, gains[:], (cs,))
+                if t == TXT_WEIGHTS_AT + 2:
+                    quantise_text_weights()
+                for u in LATE_TABLES:
+                    if u - t in TABLE_SLOTS:
+                        make_table(u, nc.vector, gains[:], (TABLE_SLOTS.index(u - t),))
                 add_bias(t + BIAS_AHEAD)
                 multiply(t)
-                if t == 0:
+                if t == 1:
                     gains_on_diagonal(nc.vector, TXT, text_banks[0][:])
+                if t == 3:
+                    gains_on_diagonal(nc.vector, IMG, gains[:])
 
-                add_and_store(t - ADD_BEHIND, (nc.gpsimd,) if is_tile(t) else (nc.gpsimd, nc.vector))
+                add_and_store(t - ADD_BEHIND)
 
-                inverse_rms(t + NORM_AHEAD)
                 sum_squares(t + SQUARES_AHEAD)
                 for u in fresh:
                     regroup(u)
+                inverse_rms(t + SQUARES_AHEAD)
                 if turned:
                     keep_trig(turned, bank)
-                if lifted is not None:
-                    keep_table(lifted)
-                if t == -1:
+                for u in lifted:
+                    keep_table(u)
+                if t == 0:
                     nc.scalar.copy(out=bias[:], in_=text_banks[1][:])
 
                 if TXT_WEIGHTS_AT <= t + 1 <= TXT_WEIGHTS_AT + 1:
                     for plane in range(2 * (t + 1 - TXT_WEIGHTS_AT), 2 * (t + 2 - TXT_WEIGHTS_AT)):
                         transpose_weight_plane(TXT, plane)
                         regroup_weight_plane(TXT, plane, nc.scalar.copy)
-                if t == TXT_WEIGHTS_AT + 1:
-                    for qk in range(2):
-                        quantise_weights(TXT, qk)
-                if odd == 0 and 0 <= t <= TXT_WEIGHTS_AT + 1:
+                if odd == 0 and 0 <= t < CATCH_UP_AT:
                     quantise_pair(pair)

@@ -23,13 +23,13 @@ S_IMG = 3072
 EPS = 1e-5
 PAIR = 2
 BEAT = 4
-FIRST_TEXT = 9
-MORE_TEXT = (23, 31)
+FIRST_TEXT = 13
+MORE_TEXT = (15, 19, 23)
 EARLY_TABLES = 8
-LATE_TABLES = (19, 27)
+LATE_TABLES = (9, 11)
 TABLE_SLOTS = (8, 6)
 
-TXT_WEIGHTS_AT = 3
+TXT_WEIGHTS_AT = 2
 TRANSPOSE_AHEAD = 7
 PROJECT_AHEAD = 3
 BIAS_AHEAD = 2
@@ -151,11 +151,12 @@ def tile_flux2attention_pa_t_kernel(
         load_trig(IMG, 0)
         load_tiles(range(4, 6))
         load_tiles(range(6, 9))
-        load_weights(TXT)
-        load_tiles(range(9, 10))
-        load_trig(TXT, 0)
         load_trig(IMG, 1)
-        load_tiles(range(10, 17))
+        load_tiles(range(9, 12))
+        load_weights(TXT)
+        load_tiles(range(12, 14))
+        load_trig(TXT, 0)
+        load_tiles(range(14, 17))
         load_trig(IMG, 2)
         load_tiles(range(17, n_all))
 
@@ -473,7 +474,7 @@ def tile_flux2attention_pa_t_kernel(
                             make_table(u, nc.vector, gains_bank[:])
                         else:
                             make_table(u, nc.gpsimd, gains[:])
-                if t == TXT_WEIGHTS_AT + 2:
+                if t == FIRST_TEXT - 4:
                     quantise_text_weights()
                 for u in LATE_TABLES:
                     if u - t in TABLE_SLOTS:
@@ -498,8 +499,8 @@ def tile_flux2attention_pa_t_kernel(
                 if t == 0:
                     nc.scalar.copy(out=bias[:], in_=text_banks[1][:])
 
-                if TXT_WEIGHTS_AT <= t + 1 <= TXT_WEIGHTS_AT + 1:
-                    for plane in range(2 * (t + 1 - TXT_WEIGHTS_AT), 2 * (t + 2 - TXT_WEIGHTS_AT)):
+                if 0 <= t - TXT_WEIGHTS_AT < PLANES:
+                    for plane in (t - TXT_WEIGHTS_AT,):
                         transpose_weight_plane(TXT, plane)
                         regroup_weight_plane(TXT, plane, nc.scalar.copy)
                 if odd == 0 and 0 <= t < CATCH_UP_AT:

@@ -90,12 +90,12 @@ def tile_flux2attention_pa_t_kernel(
 
     with ExitStack() as ctx:
         const = ctx.enter_context(tc.tile_pool(name="const", bufs=1))
-        x_pool = ctx.enter_context(tc.tile_pool(name="x_pool", bufs=n_pairs))
+        x_pool = ctx.enter_context(tc.tile_pool(name="x_pool", bufs=n_pairs - 4))
         w_pool = ctx.enter_context(tc.tile_pool(name="w_pool", bufs=4))
         ring3 = ctx.enter_context(tc.tile_pool(name="ring3", bufs=3))
         ring4 = ctx.enter_context(tc.tile_pool(name="ring4", bufs=4))
         ring6 = ctx.enter_context(tc.tile_pool(name="ring6", bufs=6))
-        out_pool = ctx.enter_context(tc.tile_pool(name="out_pool", bufs=10))
+        out_pool = ctx.enter_context(tc.tile_pool(name="out_pool", bufs=14))
         table_pool = ctx.enter_context(tc.tile_pool(name="table_pool", bufs=EARLY_TABLES))
         psum_t = ctx.enter_context(tc.psum_pool(name="psum_t", bufs=2))
         psum_y = ctx.enter_context(tc.psum_pool(name="psum_y", bufs=4))
@@ -145,9 +145,10 @@ def tile_flux2attention_pa_t_kernel(
 
         load_vectors((wq_norm, wk_norm), 2 * HEAD)
         load_weights(IMG)
+        load_tiles(range(0, 2))
         load_vectors((waq_norm, wak_norm), 0)
         load_vectors((baq, bak), OUTS)
-        load_tiles(range(0, 4))
+        load_tiles(range(2, 4))
         load_trig(IMG, 0)
         load_tiles(range(4, 6))
         load_tiles(range(6, 9))
@@ -174,7 +175,7 @@ def tile_flux2attention_pa_t_kernel(
         ordered = const.tile([P, 3, OUTS], BF16)
         nc.vector.memset(ordered[:], 0.0)
         gains = const.tile([P, OUTS], BF16)
-        bias = const.tile([P, OUTS], F32)
+        bias = const.tile([P, OUTS], BF16)
         diagonal = {s: const.tile([P, 2, 2, HEAD], BF16, name="diagonal%d" % s) for s in (IMG, TXT)}
 
         def order_gains(stream):
@@ -190,7 +191,7 @@ def tile_flux2attention_pa_t_kernel(
             nc.vector.tensor_copy(out=ordered[0:1, 2, :], in_=vectors[:, OUTS : 2 * OUTS])
 
         def spread(row):
-            bank = psum_x.tile([P, OUTS], F32, name="spread%d" % row, tag="x")
+            bank = psum_x.tile([P, OUTS], BF16, name="spread%d" % row, tag="x")
             nc.tensor.matmul(out=bank[:], lhsT=ones[:], rhs=ordered[:, row, :], start=True, stop=True)
             return bank
 
@@ -456,12 +457,12 @@ def tile_flux2attention_pa_t_kernel(
                     turned = [u for u in range(t + 3, t + 3 + BEAT) if is_text(u) or is_lifted(u)]
                 if turned:
                     bank = transpose_trig(turned)
-                lifted = {1: [t + 2], 2: [t + 3, t + 4]}.get((t - FIRST_TEXT) % BEAT, [])
+                lifted = {1: [t + 2], 2: [t + 3], 3: [t + 3]}.get((t - FIRST_TEXT) % BEAT, [])
                 lifted = [u for u in lifted if is_lifted(u)]
-                for u in lifted:
-                    project_table(u)
                 if is_text(t + 1):
                     project_table(t + 1)
+                for u in lifted:
+                    project_table(u)
                 if t == -1:
                     text_banks = (spread(TXT), spread(2))
 

from contextlib import ExitStack

import concourse.mybir as mybir
from concourse.masks import make_identity

F32 = mybir.dt.float32
BF16 = mybir.dt.bfloat16
U32 = mybir.dt.uint32
U8 = mybir.dt.uint8
FP8X4 = mybir.dt.float8_e4m3fn_x4
ACT = mybir.ActivationFunctionType
ALU = mybir.AluOpType

P = 128
K = 1024
PASSES = 2
BLOCKS = 4
HEAD = 128
OUTS = 512
PLANES = 4
S_TXT = 1024
S_IMG = 3072
EPS = 1e-5
PAIR = 2
BEAT = 4
FIRST_TEXT = 13
MORE_TEXT = (15, 19, 23)
EARLY_TABLES = 8
LATE_TABLES = (9, 11)
TABLE_SLOTS = (8, 6)

TXT_WEIGHTS_AT = 2
TRANSPOSE_AHEAD = 7
PROJECT_AHEAD = 3
BIAS_AHEAD = 2
SQUARES_AHEAD = 2
NORM_AHEAD = 1
ADD_BEHIND = 1
CATCH_UP_AT = 4
TRIG_CHUNK = 8

FLOPS = 2 * (S_TXT + S_IMG) * K * OUTS


def tile_flux2attention_pa_t_kernel(
    tc,
    hidden_states,
    encoder_hidden_states,
    rope_cos,
    rope_sin,
    Wq,
    Wk,
    Waq,
    baq,
    Wak,
    bak,
    wq_norm,
    wk_norm,
    waq_norm,
    wak_norm,
    out_0,
    out_1,
):
    nc = tc.nc
    TXT, IMG = 0, 1
    first_row = (0, S_TXT)
    n_tiles = (S_TXT // P, S_IMG // P)
    weights = ((Waq, Wak), (Wq, Wk))

    def by_partition(rows, stream):
        lo = first_row[stream]
        return rows[lo : lo + n_tiles[stream] * P, :].rearrange("(p m) c -> p m c", p=P)

    x_dram = (
        encoder_hidden_states.rearrange("b (p m) k -> p (b m) k", p=P),
        hidden_states.rearrange("b (p m) k -> p (b m) k", p=P),
    )
    q_rows = out_0.rearrange("b s h d -> (b s) (h d)")
    k_rows = out_1.rearrange("b s h d -> (b s) (h d)")
    q_dram = (by_partition(q_rows, TXT), by_partition(q_rows, IMG))
    k_dram = (by_partition(k_rows, TXT), by_partition(k_rows, IMG))

    n_all = n_tiles[TXT] + n_tiles[IMG]
    text_tiles = list(range(FIRST_TEXT, n_all, BEAT)) + list(MORE_TEXT)
    tiles = []
    for t in range(n_all):
        stream = TXT if t in text_tiles else IMG
        tiles.append((stream, len([s for s, m in tiles if s == stream])))
    n_pairs = n_all // PAIR

    with ExitStack() as ctx:
        const = ctx.enter_context(tc.tile_pool(name="const", bufs=1))
        x_pool = ctx.enter_context(tc.tile_pool(name="x_pool", bufs=n_pairs - 4))
        w_pool = ctx.enter_context(tc.tile_pool(name="w_pool", bufs=4))
        ring3 = ctx.enter_context(tc.tile_pool(name="ring3", bufs=3))
        ring4 = ctx.enter_context(tc.tile_pool(name="ring4", bufs=4))
        ring6 = ctx.enter_context(tc.tile_pool(name="ring6", bufs=6))
        out_pool = ctx.enter_context(tc.tile_pool(name="out_pool", bufs=14))
        table_pool = ctx.enter_context(tc.tile_pool(name="table_pool", bufs=EARLY_TABLES))
        psum_t = ctx.enter_context(tc.psum_pool(name="psum_t", bufs=2))
        psum_y = ctx.enter_context(tc.psum_pool(name="psum_y", bufs=4))
        psum_x = ctx.enter_context(tc.psum_pool(name="psum_x", bufs=2))

        vectors = const.tile([1, 2 * OUTS], BF16)

        def load_vectors(vecs, col):
            for vec in vecs:
                n = vec.shape[0]
                nc.sync.dma_start(out=vectors[:, col : col + n], in_=vec.unsqueeze(0))
                col += n

        w_raw = {}
        x_raw = {}
        trig = {}

        def load_weights(stream):
            for qk in range(2):
                rows = w_pool.tile([P, 2, K], BF16, name="w_raw%d%d" % (stream, qk), tag="w_raw")
                by_head = weights[stream][qk].rearrange("(h d) k -> d h k", h=2)
                for h in range(2):
                    nc.sync.dma_start(out=rows[:, h, :], in_=by_head[:, h, :])
                    w_raw[(stream, 2 * qk + h)] = rows[:, h, :]

        def load_tiles(ts):
            for t in ts:
                stream, m = tiles[t]
                if tiles[t] in x_raw:
                    continue
                rows = x_pool.tile([P, PAIR, K], BF16, name="x_raw%d" % t, tag="x_raw")
                if t == 0:
                    for n in range(PAIR):
                        nc.sync.dma_start(out=rows[:, n, :], in_=x_dram[stream][:, m + n, :])
                else:
                    nc.sync.dma_start(out=rows[:], in_=x_dram[stream][:, m : m + PAIR, :])
                for n in range(PAIR):
                    x_raw[(stream, m + n)] = rows[:, n, :]

        def load_trig(stream, chunk):
            m = chunk * TRIG_CHUNK
            both = const.tile([P, 2, TRIG_CHUNK, HEAD], BF16, name="trig%d%d" % (stream, chunk))
            for cs, rows in enumerate((rope_cos, rope_sin)):
                nc.sync.dma_start(out=both[:, cs], in_=by_partition(rows, stream)[:, m : m + TRIG_CHUNK, :])
            for n in range(TRIG_CHUNK):
                trig[(stream, m + n)] = both[:, :, n, :]

        load_vectors((wq_norm, wk_norm), 2 * HEAD)
        load_weights(IMG)
        load_tiles(range(0, 2))
        load_vectors((waq_norm, wak_norm), 0)
        load_vectors((baq, bak), OUTS)
        load_tiles(range(2, 4))
        load_trig(IMG, 0)
        load_tiles(range(4, 6))
        load_tiles(range(6, 9))
        load_trig(IMG, 1)
        load_tiles(range(9, 12))
        load_weights(TXT)
        load_tiles(range(12, 14))
        load_trig(TXT, 0)
        load_tiles(range(14, 17))
        load_trig(IMG, 2)
        load_tiles(range(17, n_all))

        one = const.tile([P, 1], F32)
        nc.vector.memset(one[:], 1.0)
        warm = const.tile([P, 1], F32)
        nc.scalar.activation(out=warm[:], in_=one[:], func=ACT.Abs_reciprocal_sqrt, bias=EPS, scale=1.0 / HEAD)
        ident = const.tile([P, P], F32)
        make_identity(nc, ident[:])
        ident_bf = const.tile([P, P], BF16)
        make_identity(nc, ident_bf[:])

        ones = const.tile([P, P], BF16)
        nc.vector.memset(ones[:], 1.0)
        ordered = const.tile([P, 3, OUTS], BF16)
        nc.vector.memset(ordered[:], 0.0)
        gains = const.tile([P, OUTS], BF16)
        bias = const.tile([P, OUTS], BF16)
        diagonal = {s: const.tile([P, 2, 2, HEAD], BF16, name="diagonal%d" % s) for s in (IMG, TXT)}

        def order_gains(stream):
            w = vectors[:, 2 * HEAD * stream : 2 * HEAD * (stream + 1)]
            g = ordered[0:1, stream, :].rearrange("p (cs c) -> p cs c", cs=2)
            pairs = w.rearrange("p (ci two) -> p ci two", two=2)
            beside_sin = g[:, 1, :].rearrange("p (ci two) -> p ci two", two=2)
            nc.vector.tensor_copy(out=g[:, 0, :], in_=w)
            nc.vector.tensor_copy(out=beside_sin[:, :, 0], in_=pairs[:, :, 0])
            nc.vector.tensor_scalar_mul(out=beside_sin[:, :, 1], in0=pairs[:, :, 1], scalar1=-1.0)

        def order_bias():
            nc.vector.tensor_copy(out=ordered[0:1, 2, :], in_=vectors[:, OUTS : 2 * OUTS])

        def spread(row):
            bank = psum_x.tile([P, OUTS], BF16, name="spread%d" % row, tag="x")
            nc.tensor.matmul(out=bank[:], lhsT=ones[:], rhs=ordered[:, row, :], start=True, stop=True)
            return bank

        def by_pair(ap):
            return ap.rearrange("p (i two) -> p i two", two=2)

        def gains_times(engine, out, row, cos, sin, parts=(0, 1)):
            for cs in parts:
                values = by_pair(cos) if cs == 0 else by_pair(sin)[:, :, ::-1]
                engine.tensor_tensor(
                    out=out[:, cs].rearrange("p q (i two) -> p q i two", two=2),
                    in0=values.unsqueeze(1).to_broadcast([P, 2, HEAD // 2, 2]),
                    in1=row.rearrange("p (cs q i two) -> p cs q i two", cs=2, q=2, two=2)[:, cs],
                    op=ALU.mult,
                )

        def gains_on_diagonal(engine, stream, row):
            gains_times(engine, diagonal[stream], row, ident_bf[:], ident_bf[:])

        w_grouped = {}
        w_t = {}
        w_codes = {}
        w_scales = {}
        x_t = {}
        x_grouped = {}
        x_codes = {}
        x_scales = {}
        trig_t = {}
        table = {}
        y = {}
        sumsq = {}
        rstd = {}
        products = {}

        def is_tile(t):
            return 0 <= t < n_all

        def is_text(t):
            return is_tile(t) and tiles[t][0] == TXT

        def is_lifted(t):
            return EARLY_TABLES <= t < n_all and not is_text(t) and t not in LATE_TABLES

        def transpose_weight_plane(stream, plane):
            qk, h = divmod(plane, 2)
            if stream == IMG and h == 0:
                half = const.tile([P, PASSES, 2 * HEAD, 4], BF16, align_bytes=64, name="w_grouped_img%d" % qk)
                w_grouped[(stream, qk)] = half[:]
            if stream == TXT and plane == 0:
                whole = const.tile([P, PASSES, OUTS, 4], BF16, align_bytes=64, name="w_grouped_txt")
                w_grouped[stream] = whole[:]
                for n in range(2):
                    w_grouped[(stream, n)] = whole[:, :, n * 2 * HEAD : (n + 1) * 2 * HEAD, :]
            words = w_raw[(stream, plane)].bitcast(F32)
            if stream == IMG:
                wt = psum_y.tile([P, BLOCKS, P], F32, name="wt", tag="y")
            else:
                wt = psum_x.tile([P, BLOCKS, P], F32, name="wt", tag="x")
            for c in range(BLOCKS):
                nc.tensor.transpose(wt[:, c, :], words[:, c * P : (c + 1) * P], ident[:])
            w_t[(stream, plane)] = wt

        def regroup_weight_plane(stream, plane, copy):
            qk, h = divmod(plane, 2)
            copy(
                out=w_grouped[(stream, qk)].bitcast(F32)[:, :, h * P : (h + 1) * P, :],
                in_=w_t[(stream, plane)][:].rearrange("p (g u) r -> p g r u", u=2),
            )

        for stream in (TXT, IMG):
            w_codes[stream] = const.tile([P, PASSES, OUTS], U32, align_bytes=64, name="w_codes%d" % stream)
            w_scales[stream] = const.tile([P, PASSES, OUTS], U8, align_bytes=64, name="w_scales%d" % stream)

        def quantise_image_weights(qk):
            cols = slice(qk * 2 * HEAD, (qk + 1) * 2 * HEAD)
            for g in range(PASSES):
                nc.vector.quantize_mx(
                    out=w_codes[IMG][:, g, cols].bitcast(FP8X4),
                    scales=w_scales[IMG][:, g, cols],
                    in_=w_grouped[(IMG, qk)][:, g].rearrange("p c j -> p (c j)"),
                )

        def quantise_text_weights():
            nc.vector.quantize_mx(
                out=w_codes[TXT][:].rearrange("p g c -> p (g c)").bitcast(FP8X4),
                scales=w_scales[TXT][:].rearrange("p g c -> p (g c)"),
                in_=w_grouped[TXT].rearrange("p g c j -> p (g c j)"),
            )

        def transpose_tile(t):
            if not is_tile(t):
                return
            pair, n = divmod(t, PAIR)
            if n == 0:
                x_grouped[pair] = ring4.tile([P, PAIR, PASSES, P, 4], BF16, align_bytes=64, name="x_grouped")
            words = x_raw[tiles[t]].bitcast(F32)
            xt = psum_t.tile([P, BLOCKS, P], F32, tag="t")
            for c in range(BLOCKS):
                nc.tensor.transpose(xt[:, c, :], words[:, c * P : (c + 1) * P], ident[:])
            x_t[t] = xt

        def regroup(t):
            if not is_tile(t):
                return
            nc.scalar.copy(
                out=x_grouped[t // PAIR][:, t % PAIR].bitcast(F32),
                in_=x_t[t][:].rearrange("p (g u) r -> p g r u", u=2),
            )

        def quantise_pair(pair):
            if not is_tile(PAIR * pair):
                return
            codes = ring3.tile([P, PAIR, PASSES, P], U32, align_bytes=64, name="x_codes")
            scales = ring3.tile([P, PAIR, PASSES, P], U8, align_bytes=64, name="x_scales")
            nc.vector.quantize_mx(
                out=codes[:].rearrange("p n g r -> p (n g r)").bitcast(FP8X4),
                scales=scales[:].rearrange("p n g r -> p (n g r)"),
                in_=x_grouped[pair][:].rearrange("p n g r j -> p (n g r j)"),
            )
            x_codes[pair] = codes
            x_scales[pair] = scales

        def project_tile(t):
            if not is_tile(t):
                return
            stream = tiles[t][0]
            pair, n = divmod(t, PAIR)
            acc = psum_y.tile([P, OUTS], F32, tag="y")
            for g in range(PASSES):
                nc.tensor.matmul_mx(
                    out=acc[:],
                    lhsT=x_codes[pair][:, n, g, :].bitcast(FP8X4),
                    lhsT_scale=x_scales[pair][:, n, g, :],
                    rhs=w_codes[stream][:, g, :].bitcast(FP8X4),
                    rhs_scale=w_scales[stream][:, g, :],
                    start=(g == 0),
                    stop=(g == PASSES - 1),
                )
            y[t] = acc

        def make_table(t, engine, row, parts=(0, 1)):
            if 0 in parts:
                table[t] = table_pool.tile([P, 2, 2, HEAD], F32, name="tab")
            gains_times(engine, table[t], row, trig[tiles[t]][:, 0, :], trig[tiles[t]][:, 1, :], parts)

        def transpose_trig(ts):
            bank = psum_x.tile([P, len(ts), 2, P], BF16, name="trig_bank", tag="x")
            for n, t in enumerate(ts):
                for cs in range(2):
                    nc.tensor.transpose(bank[:, n, cs, :], trig[tiles[t]][:, cs, :], ident_bf[:])
            return bank

        def keep_trig(ts, bank):
            kept = ring3.tile([P, BEAT, 2, P], BF16, name="trig_t")
            nc.scalar.copy(out=kept[:, : len(ts)], in_=bank[:])
            for n, t in enumerate(ts):
                trig_t[t] = kept[:, n]

        def project_table(t):
            tab = psum_x.tile([P, 2, 2, HEAD], F32, name="table_bank", tag="x")
            for cs in range(2):
                nc.tensor.matmul(
                    out=tab[:, cs].rearrange("p q d -> p (q d)"),
                    lhsT=trig_t[t][:, cs, :],
                    rhs=diagonal[tiles[t][0]][:, cs].rearrange("p q d -> p (q d)"),
                    start=True,
                    stop=True,
                )
            table[t] = tab

        def keep_table(t):
            tab = ring6.tile([P, 2, 2, HEAD], F32, name="kept_table")
            nc.scalar.copy(out=tab[:], in_=table[t][:])
            table[t] = tab

        def add_bias(t):
            if not is_text(t):
                return
            biased = ring4.tile([P, OUTS], F32, name="biased")
            nc.vector.tensor_tensor(out=biased[:], in0=y[t][:], in1=bias[:], op=ALU.add)
            y[t] = biased

        def sum_squares(t):
            if not is_tile(t):
                return
            squares = ring3.tile([P, OUTS], BF16, name="squares")
            sums = ring6.tile([P, PLANES], F32, name="sums")
            for v in range(PLANES):
                nc.scalar.activation(
                    out=squares[:, v * HEAD : (v + 1) * HEAD],
                    in_=y[t][:, v * HEAD : (v + 1) * HEAD],
                    func=ACT.Square,
                    accum_out=sums[:, v : v + 1],
                )
            sumsq[t] = sums

        def inverse_rms(t):
            if not is_tile(t):
                return
            r = ring6.tile([P, PLANES], F32, name="r")
            nc.scalar.activation(out=r[:], in_=sumsq[t][:], func=ACT.Abs_reciprocal_sqrt, bias=EPS, scale=1.0 / HEAD)
            rstd[t] = r

        def multiply(t):
            if not is_tile(t):
                return
            both = ring3.tile([P, 2, PLANES, HEAD], F32, name="both")
            for v in range(PLANES):
                nc.vector.scalar_tensor_tensor(
                    out=both[:, :, v, :],
                    in0=y[t][:, v * HEAD : (v + 1) * HEAD].unsqueeze(1).to_broadcast([P, 2, HEAD]),
                    scalar=rstd[t][:, v : v + 1],
                    in1=table[t][:, :, v // 2, :],
                    op0=ALU.mult,
                    op1=ALU.mult,
                )
            products[t] = both

        def add_and_store(t):
            if not is_tile(t):
                return
            stream, m = tiles[t]
            result = out_pool.tile([P, OUTS], F32, name="result")
            straight, crossed = (products[t][:, n].rearrange("p v d -> p (v d)") for n in range(2))
            last = t == n_all - 1
            halves = [slice(0, 2 * HEAD), slice(2 * HEAD, OUTS)]
            for cols in halves if last else [slice(0, OUTS)]:
                (nc.vector if last else nc.gpsimd).tensor_tensor(
                    out=by_pair(result[:, cols]),
                    in0=by_pair(straight[:, cols]),
                    in1=by_pair(crossed[:, cols])[:, :, ::-1],
                    op=ALU.add,
                )
            for rows, cols in zip((q_dram, k_dram), halves):
                nc.sync.dma_start(out=rows[stream][:, m, :], in_=result[:, cols])

        with tc.manual_schedule():
            order_gains(IMG)
            gains_bank = spread(IMG)
            nc.vector.tensor_copy(out=gains[:], in_=gains_bank[:])
            for plane in range(PLANES):
                transpose_weight_plane(IMG, plane)
                if plane % 2 == 0:
                    regroup_weight_plane(IMG, plane, nc.scalar.copy)
                else:
                    regroup_weight_plane(IMG, plane, nc.vector.tensor_copy)
                    quantise_image_weights(plane // 2)
            order_gains(TXT)
            order_bias()
            for t in range(-TRANSPOSE_AHEAD, n_all + ADD_BEHIND):
                if t < -PROJECT_AHEAD:
                    fresh = [t + TRANSPOSE_AHEAD]
                elif t <= CATCH_UP_AT:
                    fresh = [t + TRANSPOSE_AHEAD - 1] if t > -PROJECT_AHEAD else []
                    fresh += [t + TRANSPOSE_AHEAD] if t == CATCH_UP_AT else []
                else:
                    fresh = [t + TRANSPOSE_AHEAD]
                for u in fresh:
                    transpose_tile(u)
                project_tile(t + PROJECT_AHEAD)
                turned = []
                if t % BEAT == FIRST_TEXT % BEAT:
                    turned = [u for u in range(t + 3, t + 3 + BEAT) if is_text(u) or is_lifted(u)]
                if turned:
                    bank = transpose_trig(turned)
                lifted = {1: [t + 2], 2: [t + 3], 3: [t + 3]}.get((t - FIRST_TEXT) % BEAT, [])
                lifted = [u for u in lifted if is_lifted(u)]
                if is_text(t + 1):
                    project_table(t + 1)
                for u in lifted:
                    project_table(u)
                if t == -1:
                    text_banks = (spread(TXT), spread(2))

                pair, odd = divmod(t + 1 + PROJECT_AHEAD, PAIR)
                if odd == 0 and not 0 <= t < CATCH_UP_AT:
                    quantise_pair(pair)
                if t == -PROJECT_AHEAD - 1:
                    for u in range(EARLY_TABLES):
                        if u < EARLY_TABLES // 2:
                            make_table(u, nc.vector, gains_bank[:])
                        else:
                            make_table(u, nc.gpsimd, gains[:])
                if t == FIRST_TEXT - 4:
                    quantise_text_weights()
                for u in LATE_TABLES:
                    if u - t in TABLE_SLOTS:
                        make_table(u, nc.vector, gains[:], (TABLE_SLOTS.index(u - t),))
                add_bias(t + BIAS_AHEAD)
                multiply(t)
                if t == 1:
                    gains_on_diagonal(nc.vector, TXT, text_banks[0][:])
                if t == 3:
                    gains_on_diagonal(nc.vector, IMG, gains[:])

                add_and_store(t - ADD_BEHIND)

                sum_squares(t + SQUARES_AHEAD)
                for u in fresh:
                    regroup(u)
                inverse_rms(t + SQUARES_AHEAD)
                if turned:
                    keep_trig(turned, bank)
                for u in lifted:
                    keep_table(u)
                if t == 0:
                    nc.scalar.copy(out=bias[:], in_=text_banks[1][:])

                if 0 <= t - TXT_WEIGHTS_AT < PLANES:
                    for plane in (t - TXT_WEIGHTS_AT,):
                        transpose_weight_plane(TXT, plane)
                        regroup_weight_plane(TXT, plane, nc.scalar.copy)
                if odd == 0 and 0 <= t < CATCH_UP_AT:
                    quantise_pair(pair)
